import numpy as np
import ml_dtypes


def mxq(x, axis, fmt="e4m3"):
    dtype, down = {"e4m3": (ml_dtypes.float8_e4m3fn, 7), "e5m2": (ml_dtypes.float8_e5m2, 14)}[fmt]
    v = np.moveaxis(np.asarray(x, np.float32).astype(ml_dtypes.bfloat16).astype(np.float64), axis, -1)
    blocks = v.reshape(v.shape[:-1] + (-1, 32))
    amax = np.abs(blocks).max(-1, keepdims=True)
    byte = np.maximum(np.where(amax > 0, np.frexp(amax)[1] - 1 + 127, 0) - down, 1)
    scale = np.exp2(byte - 127.0)
    codes = (blocks / scale).astype(np.float32).astype(dtype).astype(np.float64)
    return np.moveaxis((codes * scale).reshape(v.shape), -1, axis)


WIDE = False


def mx_kscale(k):
    if not WIDE:
        return np.ones(k)
    levels = np.array([10, -10, 5, -5, 0])
    a = np.random.permutation(np.resize(levels, k // 512 * 4)).reshape(k // 512, 4)
    idx = np.arange(k)
    return np.exp2(a[idx // 512, idx % 128 // 32])


BF16 = ml_dtypes.bfloat16


def bf(x):
    return np.asarray(x, np.float32).astype(BF16)


def f64(x):
    return np.asarray(x).astype(np.float64)


B, H, W, C, F, KH, KW, G, P = 2, 8, 8, 64, 256, 3, 3, 5, 3
HO, WO = H - KH + 1, W - KW + 1
NB = G + P
IN = KH * KW * C
GRID_MIN, GRID_MAX = -1.0, 1.0


def knots():
    h = (GRID_MAX - GRID_MIN) / G
    return np.linspace(GRID_MIN - P * h, GRID_MAX + P * h, G + 2 * P + 1)


def spline_basis(v):
    t = knots()
    v = v[..., None]
    b = np.where((v >= t[:-1]) & (v < t[1:]), 1.0, 0.0)
    for k in range(1, P + 1):
        b = ((v - t[:-(k + 1)]) / (t[k:-1] - t[:-(k + 1)]) * b[..., :-1]
             + (t[k + 1:] - v) / (t[k + 1:] - t[1:-k]) * b[..., 1:])
    return b


def setup_inputs():
    t = knots()
    a = np.maximum(np.log2(mx_kscale(C * NB)[::NB]), 0.0)
    x0 = np.random.standard_normal((B, H, W, C))
    sgn = np.where(np.random.standard_normal((B, H, W, C)) < 0.0, -1.0, 1.0)
    edge = sgn * (t[-1] - (t[1] - t[0]) * 2.0 ** (-a / 2.0))
    x = bf(np.where(a > 0.0, edge, x0))
    peak = spline_basis(f64(x)).max(axis=-1).reshape(B * H * W, C).max(axis=0)
    r = np.where(a > 0.0, 2.0 ** np.round(-np.log2(peak)), 1.0)
    rows = np.tile(r, KH * KW)
    return {"x": x,
            "spline_kernel": bf(np.random.standard_normal((IN, NB, F)) * rows[:, None, None]),
            "scale_factor": bf(np.random.standard_normal((IN, F)) / np.sqrt(IN)),
            "base": bf(np.random.standard_normal((B, HO, WO, F)) * 0.6),
            "kan_bias": bf(np.random.standard_normal(F) * 0.2),
            "conv_bias": bf(np.random.standard_normal(F) * 0.2)}


def reference(x, spline_kernel, scale_factor, base, kan_bias, conv_bias):
    sb = spline_basis(f64(x))
    sq = mxq(sb.reshape(B * H * W, C * NB), 1, "e4m3").reshape(B, H, W, C * NB)
    w = f64(spline_kernel) * f64(scale_factor)[:, None, :]
    wq = mxq(w.reshape(KH * KW, C * NB, F), 1, "e4m3")
    spl = 0.0
    for di in range(KH):
        for dj in range(KW):
            win = sq[:, di:di + HO, dj:dj + WO, :].reshape(B * HO * WO, C * NB)
            spl = spl + (win @ wq[di * KW + dj])
    out = spl.reshape(B, HO, WO, F) + f64(base) + f64(kan_bias)
    return out + f64(conv_bias)

@@ -1,0 +1,172 @@
+from contextlib import ExitStack
+
+import concourse.mybir as mybir
+from concourse.masks import make_identity
+
+F32 = mybir.dt.float32
+BF16 = mybir.dt.bfloat16
+I32 = mybir.dt.int32
+U32 = mybir.dt.uint32
+U8 = mybir.dt.uint8
+FP8X4 = mybir.dt.float8_e4m3fn_x4
+ALU = mybir.AluOpType
+ACT = mybir.ActivationFunctionType
+
+P = 128
+PACK = 4
+IMAGES, HEIGHT, WIDTH, CHANNELS = 2, 8, 8, 64
+KERNEL = 3
+TAPS = KERNEL * KERNEL
+OUT_SIDE = HEIGHT - KERNEL + 1
+FILTERS = 256
+POSITIONS = IMAGES * HEIGHT * WIDTH
+ROWS = IMAGES * OUT_SIDE * OUT_SIDE
+HALVES = 2
+STORE_SPLIT = 64
+
+FLOPS = 2 * ROWS * TAPS * CHANNELS * 8 * FILTERS
+
+
+def tile_conv2dkan_pa_s_kernel(
+    tc, x, spline_kernel, scale_factor, base, kan_bias, conv_bias, out
+):
+    nc = tc.nc
+    with ExitStack() as stack:
+        keep = stack.enter_context(tc.tile_pool(name="keep", bufs=1))
+        psum = stack.enter_context(tc.psum_pool(name="psum", bufs=1))
+
+        ident = keep.tile([P, P], F32)
+        make_identity(nc, ident[:])
+        shift = keep.tile([P, PACK], F32)
+        for j in range(PACK):
+            nc.gpsimd.memset(shift[:, j : j + 1], float(j))
+        ones = keep.tile([P, P], BF16)
+        nc.gpsimd.memset(ones[:], 1.0)
+        bias_rows = keep.tile([P, FILTERS], BF16)
+        nc.vector.memset(bias_rows[:].bitcast(I32), 0)
+        patches = keep.tile([P, TAPS, P * PACK], BF16, align_bytes=64)
+        nc.vector.memset(patches[:].bitcast(I32)[:, :, ROWS * PACK // 2 :], 0)
+        warm = keep.tile([P, 1], F32)
+        nc.scalar.activation(out=warm[:], in_=shift[:, 0:1], func=ACT.Abs)
+
+        x_sb = keep.tile([P, CHANNELS], BF16)
+        nc.sync.dma_start(out=x_sb[:], in_=x.rearrange("b h w c -> (b h w) c"))
+        factor = keep.tile([P, TAPS, FILTERS], BF16)
+        factor_rows = scale_factor.rearrange("(t c) f -> c t f", t=TAPS)
+        raw = keep.tile([P, TAPS, PACK, FILTERS], BF16)
+        raw_rows = spline_kernel.rearrange("(t c) k f -> t (c k) f", t=TAPS)
+
+        def load_factor(first, last):
+            for h in range(HALVES):
+                nc.sync.dma_start(
+                    out=factor[h:P:HALVES, first:last, :], in_=factor_rows[:, first:last, :]
+                )
+
+        def load_raw(tap):
+            nc.sync.dma_start(
+                out=raw[:, tap], in_=raw_rows[tap].rearrange("(p j) f -> p j f", j=PACK)
+            )
+
+        load_factor(0, 1)
+        load_raw(0)
+        load_factor(1, TAPS)
+        for tap in range(1, TAPS):
+            load_raw(tap)
+        nc.scalar.dma_start(out=bias_rows[0:1, :], in_=kan_bias.rearrange("(o f) -> o f", o=1))
+        nc.scalar.dma_start(out=bias_rows[1:2, :], in_=conv_bias.rearrange("(o f) -> o f", o=1))
+        base_sb = keep.tile([ROWS, FILTERS], BF16)
+        nc.scalar.dma_start(out=base_sb[:], in_=base.rearrange("b p q f -> (b p q) f"))
+
+        centred = keep.tile([P, CHANNELS, HALVES], F32)
+        for h in range(HALVES):
+            nc.vector.tensor_scalar(
+                out=centred[:, :, h], in0=x_sb[:], scalar1=2.5, scalar2=3.5 - PACK * h,
+                op0=ALU.mult, op1=ALU.add,
+            )
+        centred_t = psum.tile([P, POSITIONS], F32)
+        nc.tensor.transpose(centred_t[:], centred[:].rearrange("p c h -> p (c h)"), ident[:])
+        wide = [P, POSITIONS, PACK]
+        offset = keep.tile(wide, F32)
+        nc.vector.tensor_tensor(
+            out=offset[:], in0=centred_t[:].unsqueeze(2).to_broadcast(wide),
+            in1=shift[:].unsqueeze(1).to_broadcast(wide), op=ALU.subtract,
+        )
+        dist = keep.tile(wide, F32)
+        nc.scalar.activation(out=dist[:], in_=offset[:], func=ACT.Abs)
+        outer = keep.tile(wide, F32)
+        nc.scalar.activation(out=outer[:], in_=dist[:], func=ACT.Relu, bias=2.0, scale=-1.0)
+        inner = keep.tile(wide, F32)
+        nc.scalar.activation(out=inner[:], in_=dist[:], func=ACT.Relu, bias=1.0, scale=-1.0)
+        outer_sq = keep.tile(wide, F32)
+        nc.scalar.activation(out=outer_sq[:], in_=outer[:], func=ACT.Square)
+        inner_sq = keep.tile(wide, F32)
+        nc.scalar.activation(out=inner_sq[:], in_=inner[:], func=ACT.Square)
+        outer_cube = keep.tile(wide, F32)
+        nc.vector.scalar_tensor_tensor(
+            out=outer_cube[:], in0=outer_sq[:], scalar=1.0 / 6.0, in1=outer[:],
+            op0=ALU.mult, op1=ALU.mult,
+        )
+        inner_cube = keep.tile(wide, F32)
+        nc.vector.scalar_tensor_tensor(
+            out=inner_cube[:], in0=inner_sq[:], scalar=-2.0 / 3.0, in1=inner[:],
+            op0=ALU.mult, op1=ALU.mult,
+        )
+        basis = keep.tile([P, POSITIONS * PACK], BF16)
+        nc.vector.tensor_tensor(
+            out=basis[:], in0=outer_cube[:].rearrange("p n j -> p (n j)"),
+            in1=inner_cube[:].rearrange("p n j -> p (n j)"), op=ALU.add,
+        )
+
+        run = OUT_SIDE * PACK
+        basis_rows = basis[:].rearrange("p (b r sj) -> p b r sj", b=IMAGES, r=HEIGHT)
+        for tap in range(TAPS):
+            di, dj = divmod(tap, KERNEL)
+            nc.vector.tensor_copy(
+                out=patches[:, tap, 0 : ROWS * PACK].rearrange(
+                    "p (b r sj) -> p b r sj", b=IMAGES, r=OUT_SIDE
+                ),
+                in_=basis_rows[:, :, di : di + OUT_SIDE, dj * PACK : dj * PACK + run],
+            )
+        patch_codes = keep.tile([P, TAPS, P], U32, align_bytes=64)
+        patch_scales = keep.tile([P, TAPS, P], U8, align_bytes=64)
+        for tap in range(TAPS):
+            nc.vector.quantize_mx(
+                out=patch_codes[:, tap, :].bitcast(FP8X4), scales=patch_scales[:, tap, :],
+                in_=patches[:, tap, :],
+            )
+
+        bias_sum = psum.tile([P, FILTERS], F32)
+        nc.tensor.matmul(bias_sum[:], lhsT=ones[:], rhs=bias_rows[:], start=True, stop=True)
+        addend = keep.tile([ROWS, FILTERS], F32)
+        nc.vector.tensor_tensor(out=addend[:], in0=bias_sum[0:ROWS, :], in1=base_sb[:], op=ALU.add)
+
+        weight = keep.tile([P, TAPS, PACK, FILTERS], BF16)
+        grouped = keep.tile([P, TAPS, FILTERS, PACK], BF16, align_bytes=64)
+        weight_codes = keep.tile([P, TAPS, FILTERS], U32, align_bytes=64)
+        weight_scales = keep.tile([P, TAPS, FILTERS], U8, align_bytes=64)
+        acc = psum.tile([P, FILTERS], F32)
+        for tap in range(TAPS):
+            nc.vector.tensor_tensor(
+                out=weight[:, tap], in0=raw[:, tap],
+                in1=factor[:, tap, :].unsqueeze(1).to_broadcast([P, PACK, FILTERS]), op=ALU.mult,
+            )
+            nc.scalar.copy(
+                out=grouped[:, tap].rearrange("p (c i) j -> p c j i", i=4),
+                in_=weight[:, tap].rearrange("p j (c i) -> p c j i", i=4),
+            )
+            nc.vector.quantize_mx(
+                out=weight_codes[:, tap, :].bitcast(FP8X4), scales=weight_scales[:, tap, :],
+                in_=grouped[:, tap].rearrange("p f j -> p (f j)"),
+            )
+            nc.tensor.matmul_mx(
+                out=acc[:],
+                lhsT=patch_codes[:, tap, :].bitcast(FP8X4), lhsT_scale=patch_scales[:, tap, :],
+                rhs=weight_codes[:, tap, :].bitcast(FP8X4), rhs_scale=weight_scales[:, tap, :],
+                start=(tap == 0), stop=(tap == TAPS - 1),
+            )
+
+        result = keep.tile([ROWS, FILTERS], F32)
+        nc.vector.tensor_tensor(out=result[:], in0=acc[0:ROWS, :], in1=addend[:], op=ALU.add)
+        out_rows = out.rearrange("b p q f -> (b p q) f")
+        nc.sync.dma_start(out=out_rows[0:STORE_SPLIT, :], in_=result[0:STORE_SPLIT, :])
+        nc.scalar.dma_start(out=out_rows[STORE_SPLIT:ROWS, :], in_=result[STORE_SPLIT:ROWS, :])

@@ -22,6 +22,7 @@ FILTERS = 256
 POSITIONS = IMAGES * HEIGHT * WIDTH
 ROWS = IMAGES * OUT_SIDE * OUT_SIDE
 HALVES = 2
+EARLY_TAPS = 3
 STORE_SPLIT = 64
 
 FLOPS = 2 * ROWS * TAPS * CHANNELS * 8 * FILTERS
@@ -34,20 +35,16 @@ def tile_conv2dkan_pa_s_kernel(
     with ExitStack() as stack:
         keep = stack.enter_context(tc.tile_pool(name="keep", bufs=1))
         psum = stack.enter_context(tc.psum_pool(name="psum", bufs=1))
+        stack.enter_context(tc.manual_schedule())
 
         ident = keep.tile([P, P], F32)
         make_identity(nc, ident[:])
-        shift = keep.tile([P, PACK], F32)
-        for j in range(PACK):
-            nc.gpsimd.memset(shift[:, j : j + 1], float(j))
         ones = keep.tile([P, P], BF16)
         nc.gpsimd.memset(ones[:], 1.0)
         bias_rows = keep.tile([P, FILTERS], BF16)
         nc.vector.memset(bias_rows[:].bitcast(I32), 0)
         patches = keep.tile([P, TAPS, P * PACK], BF16, align_bytes=64)
         nc.vector.memset(patches[:].bitcast(I32)[:, :, ROWS * PACK // 2 :], 0)
-        warm = keep.tile([P, 1], F32)
-        nc.scalar.activation(out=warm[:], in_=shift[:, 0:1], func=ACT.Abs)
 
         x_sb = keep.tile([P, CHANNELS], BF16)
         nc.sync.dma_start(out=x_sb[:], in_=x.rearrange("b h w c -> (b h w) c"))
@@ -77,6 +74,25 @@ def tile_conv2dkan_pa_s_kernel(
         base_sb = keep.tile([ROWS, FILTERS], BF16)
         nc.scalar.dma_start(out=base_sb[:], in_=base.rearrange("b p q f -> (b p q) f"))
 
+        warm = keep.tile([P, 1], F32)
+        nc.vector.memset(warm[:], 0.0)
+        nc.scalar.activation(out=warm[:], in_=warm[:], func=ACT.Abs)
+
+        weight = keep.tile([P, TAPS, PACK, FILTERS], BF16)
+        grouped = keep.tile([P, TAPS, FILTERS, PACK], BF16, align_bytes=64)
+
+        def multiply(tap):
+            nc.vector.tensor_tensor(
+                out=weight[:, tap], in0=raw[:, tap],
+                in1=factor[:, tap, :].unsqueeze(1).to_broadcast([P, PACK, FILTERS]), op=ALU.mult,
+            )
+
+        def regroup(tap):
+            nc.scalar.copy(
+                out=grouped[:, tap].rearrange("p (c i) j -> p c j i", i=4),
+                in_=weight[:, tap].rearrange("p j (c i) -> p c j i", i=4),
+            )
+
         centred = keep.tile([P, CHANNELS, HALVES], F32)
         for h in range(HALVES):
             nc.vector.tensor_scalar(
@@ -85,40 +101,54 @@ def tile_conv2dkan_pa_s_kernel(
             )
         centred_t = psum.tile([P, POSITIONS], F32)
         nc.tensor.transpose(centred_t[:], centred[:].rearrange("p c h -> p (c h)"), ident[:])
-        wide = [P, POSITIONS, PACK]
-        offset = keep.tile(wide, F32)
-        nc.vector.tensor_tensor(
-            out=offset[:], in0=centred_t[:].unsqueeze(2).to_broadcast(wide),
-            in1=shift[:].unsqueeze(1).to_broadcast(wide), op=ALU.subtract,
+        multiply(0)
+        planes = [P, PACK, POSITIONS]
+        dist = keep.tile(planes, F32)
+        for j in range(PACK):
+            nc.scalar.activation(out=dist[:, j, :], in_=centred_t[:], func=ACT.Abs, bias=-float(j))
+        outer_sq = keep.tile(planes, F32)
+        nc.scalar.activation(out=outer_sq[:], in_=dist[:], func=ACT.Square, bias=2.0, scale=-1.0)
+        inner_sq = keep.tile(planes, F32)
+        nc.scalar.activation(out=inner_sq[:], in_=dist[:], func=ACT.Square, bias=1.0, scale=-1.0)
+        regroup(0)
+        outer_neg = keep.tile(planes, F32)
+        nc.vector.tensor_scalar(
+            out=outer_neg[:], in0=dist[:], scalar1=2.0, scalar2=-2.0, op0=ALU.min, op1=ALU.add
         )
-        dist = keep.tile(wide, F32)
-        nc.scalar.activation(out=dist[:], in_=offset[:], func=ACT.Abs)
-        outer = keep.tile(wide, F32)
-        nc.scalar.activation(out=outer[:], in_=dist[:], func=ACT.Relu, bias=2.0, scale=-1.0)
-        inner = keep.tile(wide, F32)
-        nc.scalar.activation(out=inner[:], in_=dist[:], func=ACT.Relu, bias=1.0, scale=-1.0)
-        outer_sq = keep.tile(wide, F32)
-        nc.scalar.activation(out=outer_sq[:], in_=outer[:], func=ACT.Square)
-        inner_sq = keep.tile(wide, F32)
-        nc.scalar.activation(out=inner_sq[:], in_=inner[:], func=ACT.Square)
-        outer_cube = keep.tile(wide, F32)
+        inner_neg = keep.tile(planes, F32)
+        nc.vector.tensor_scalar(
+            out=inner_neg[:], in0=dist[:], scalar1=1.0, scalar2=-1.0, op0=ALU.min, op1=ALU.add
+        )
+        for tap in range(1, EARLY_TAPS):
+            multiply(tap)
+            regroup(tap)
+        flat = "p j n -> p (j n)"
+        outer_term = keep.tile(planes, F32)
         nc.vector.scalar_tensor_tensor(
-            out=outer_cube[:], in0=outer_sq[:], scalar=1.0 / 6.0, in1=outer[:],
-            op0=ALU.mult, op1=ALU.mult,
+            out=outer_term[:].rearrange(flat), in0=outer_sq[:].rearrange(flat), scalar=-1.0 / 6.0,
+            in1=outer_neg[:].rearrange(flat), op0=ALU.mult, op1=ALU.mult,
         )
-        inner_cube = keep.tile(wide, F32)
+        inner_term = keep.tile(planes, F32)
         nc.vector.scalar_tensor_tensor(
-            out=inner_cube[:], in0=inner_sq[:], scalar=-2.0 / 3.0, in1=inner[:],
-            op0=ALU.mult, op1=ALU.mult,
+            out=inner_term[:].rearrange(flat), in0=inner_sq[:].rearrange(flat), scalar=2.0 / 3.0,
+            in1=inner_neg[:].rearrange(flat), op0=ALU.mult, op1=ALU.mult,
         )
-        basis = keep.tile([P, POSITIONS * PACK], BF16)
+        basis = keep.tile([P, POSITIONS, PACK], BF16)
         nc.vector.tensor_tensor(
-            out=basis[:], in0=outer_cube[:].rearrange("p n j -> p (n j)"),
-            in1=inner_cube[:].rearrange("p n j -> p (n j)"), op=ALU.add,
+            out=basis[:], in0=outer_term[:].rearrange("p j n -> p n j"),
+            in1=inner_term[:].rearrange("p j n -> p n j"), op=ALU.add,
         )
+        for tap in range(EARLY_TAPS, TAPS):
+            multiply(tap)
+            regroup(tap)
+
+        bias_sum = psum.tile([P, FILTERS], F32)
+        nc.tensor.matmul(bias_sum[:], lhsT=ones[:], rhs=bias_rows[:], start=True, stop=True)
+        addend = keep.tile([ROWS, FILTERS], F32)
+        nc.vector.tensor_tensor(out=addend[:], in0=bias_sum[0:ROWS, :], in1=base_sb[:], op=ALU.add)
 
         run = OUT_SIDE * PACK
-        basis_rows = basis[:].rearrange("p (b r sj) -> p b r sj", b=IMAGES, r=HEIGHT)
+        basis_rows = basis[:].rearrange("p (b r s) j -> p b r (s j)", b=IMAGES, r=HEIGHT)
         for tap in range(TAPS):
             di, dj = divmod(tap, KERNEL)
             nc.vector.tensor_copy(
@@ -135,25 +165,10 @@ def tile_conv2dkan_pa_s_kernel(
                 in_=patches[:, tap, :],
             )
 
-        bias_sum = psum.tile([P, FILTERS], F32)
-        nc.tensor.matmul(bias_sum[:], lhsT=ones[:], rhs=bias_rows[:], start=True, stop=True)
-        addend = keep.tile([ROWS, FILTERS], F32)
-        nc.vector.tensor_tensor(out=addend[:], in0=bias_sum[0:ROWS, :], in1=base_sb[:], op=ALU.add)
-
-        weight = keep.tile([P, TAPS, PACK, FILTERS], BF16)
-        grouped = keep.tile([P, TAPS, FILTERS, PACK], BF16, align_bytes=64)
         weight_codes = keep.tile([P, TAPS, FILTERS], U32, align_bytes=64)
         weight_scales = keep.tile([P, TAPS, FILTERS], U8, align_bytes=64)
         acc = psum.tile([P, FILTERS], F32)
         for tap in range(TAPS):
-            nc.vector.tensor_tensor(
-                out=weight[:, tap], in0=raw[:, tap],
-                in1=factor[:, tap, :].unsqueeze(1).to_broadcast([P, PACK, FILTERS]), op=ALU.mult,
-            )
-            nc.scalar.copy(
-                out=grouped[:, tap].rearrange("p (c i) j -> p c j i", i=4),
-                in_=weight[:, tap].rearrange("p j (c i) -> p c j i", i=4),
-            )
             nc.vector.quantize_mx(
                 out=weight_codes[:, tap, :].bitcast(FP8X4), scales=weight_scales[:, tap, :],
                 in_=grouped[:, tap].rearrange("p f j -> p (f j)"),

@@ -22,7 +22,8 @@ FILTERS = 256
 POSITIONS = IMAGES * HEIGHT * WIDTH
 ROWS = IMAGES * OUT_SIDE * OUT_SIDE
 HALVES = 2
-EARLY_TAPS = 3
+PAIR = 2
+PATCH_CALL = 8
 STORE_SPLIT = 64
 
 FLOPS = 2 * ROWS * TAPS * CHANNELS * 8 * FILTERS
@@ -37,17 +38,8 @@ def tile_conv2dkan_pa_s_kernel(
         psum = stack.enter_context(tc.psum_pool(name="psum", bufs=1))
         stack.enter_context(tc.manual_schedule())
 
-        ident = keep.tile([P, P], F32)
-        make_identity(nc, ident[:])
-        ones = keep.tile([P, P], BF16)
-        nc.gpsimd.memset(ones[:], 1.0)
-        bias_rows = keep.tile([P, FILTERS], BF16)
-        nc.vector.memset(bias_rows[:].bitcast(I32), 0)
-        patches = keep.tile([P, TAPS, P * PACK], BF16, align_bytes=64)
-        nc.vector.memset(patches[:].bitcast(I32)[:, :, ROWS * PACK // 2 :], 0)
-
         x_sb = keep.tile([P, CHANNELS], BF16)
-        nc.sync.dma_start(out=x_sb[:], in_=x.rearrange("b h w c -> (b h w) c"))
+        nc.scalar.dma_start(out=x_sb[:], in_=x.rearrange("b h w c -> (b h w) c"))
         factor = keep.tile([P, TAPS, FILTERS], BF16)
         factor_rows = scale_factor.rearrange("(t c) f -> c t f", t=TAPS)
         raw = keep.tile([P, TAPS, PACK, FILTERS], BF16)
@@ -69,11 +61,19 @@ def tile_conv2dkan_pa_s_kernel(
         load_factor(1, TAPS)
         for tap in range(1, TAPS):
             load_raw(tap)
-        nc.scalar.dma_start(out=bias_rows[0:1, :], in_=kan_bias.rearrange("(o f) -> o f", o=1))
-        nc.scalar.dma_start(out=bias_rows[1:2, :], in_=conv_bias.rearrange("(o f) -> o f", o=1))
-        base_sb = keep.tile([ROWS, FILTERS], BF16)
-        nc.scalar.dma_start(out=base_sb[:], in_=base.rearrange("b p q f -> (b p q) f"))
 
+        ident = keep.tile([P, P], F32)
+        make_identity(nc, ident[:])
+        ones = keep.tile([P, P], BF16)
+        nc.gpsimd.memset(ones[:], 1.0)
+        bias_rows = keep.tile([P, FILTERS], BF16)
+        nc.vector.memset(bias_rows[:].bitcast(I32), 0)
+        nc.gpsimd.dma_start(out=bias_rows[0:1, :], in_=kan_bias.rearrange("(o f) -> o f", o=1))
+        nc.gpsimd.dma_start(out=bias_rows[1:2, :], in_=conv_bias.rearrange("(o f) -> o f", o=1))
+        base_sb = keep.tile([ROWS, FILTERS], BF16)
+        nc.gpsimd.dma_start(out=base_sb[:], in_=base.rearrange("b p q f -> (b p q) f"))
+        patches = keep.tile([P, TAPS, P * PACK], BF16, align_bytes=64)
+        nc.vector.memset(patches[:].bitcast(I32)[:, :, ROWS * PACK // 2 :], 0)
         warm = keep.tile([P, 1], F32)
         nc.vector.memset(warm[:], 0.0)
         nc.scalar.activation(out=warm[:], in_=warm[:], func=ACT.Abs)
@@ -81,10 +81,12 @@ def tile_conv2dkan_pa_s_kernel(
         weight = keep.tile([P, TAPS, PACK, FILTERS], BF16)
         grouped = keep.tile([P, TAPS, FILTERS, PACK], BF16, align_bytes=64)
 
-        def multiply(tap):
+        def multiply(first, count):
+            taps = slice(first, first + count)
             nc.vector.tensor_tensor(
-                out=weight[:, tap], in0=raw[:, tap],
-                in1=factor[:, tap, :].unsqueeze(1).to_broadcast([P, PACK, FILTERS]), op=ALU.mult,
+                out=weight[:, taps], in0=raw[:, taps],
+                in1=factor[:, taps, :].unsqueeze(2).to_broadcast([P, count, PACK, FILTERS]),
+                op=ALU.mult,
             )
 
         def regroup(tap):
@@ -101,7 +103,7 @@ def tile_conv2dkan_pa_s_kernel(
             )
         centred_t = psum.tile([P, POSITIONS], F32)
         nc.tensor.transpose(centred_t[:], centred[:].rearrange("p c h -> p (c h)"), ident[:])
-        multiply(0)
+        multiply(0, 1)
         planes = [P, PACK, POSITIONS]
         dist = keep.tile(planes, F32)
         for j in range(PACK):
@@ -119,9 +121,13 @@ def tile_conv2dkan_pa_s_kernel(
         nc.vector.tensor_scalar(
             out=inner_neg[:], in0=dist[:], scalar1=1.0, scalar2=-1.0, op0=ALU.min, op1=ALU.add
         )
-        for tap in range(1, EARLY_TAPS):
-            multiply(tap)
-            regroup(tap)
+
+        def multiply_and_regroup_pair(first):
+            multiply(first, PAIR)
+            for tap in range(first, first + PAIR):
+                regroup(tap)
+
+        multiply_and_regroup_pair(1)
         flat = "p j n -> p (j n)"
         outer_term = keep.tile(planes, F32)
         nc.vector.scalar_tensor_tensor(
@@ -138,9 +144,8 @@ def tile_conv2dkan_pa_s_kernel(
             out=basis[:], in0=outer_term[:].rearrange("p j n -> p n j"),
             in1=inner_term[:].rearrange("p j n -> p n j"), op=ALU.add,
         )
-        for tap in range(EARLY_TAPS, TAPS):
-            multiply(tap)
-            regroup(tap)
+        for first in range(1 + PAIR, TAPS, PAIR):
+            multiply_and_regroup_pair(first)
 
         bias_sum = psum.tile([P, FILTERS], F32)
         nc.tensor.matmul(bias_sum[:], lhsT=ones[:], rhs=bias_rows[:], start=True, stop=True)
@@ -159,26 +164,32 @@ def tile_conv2dkan_pa_s_kernel(
             )
         patch_codes = keep.tile([P, TAPS, P], U32, align_bytes=64)
         patch_scales = keep.tile([P, TAPS, P], U8, align_bytes=64)
-        for tap in range(TAPS):
+        join = "p t e -> p (t e)"
+        for first in range(0, TAPS, PATCH_CALL):
+            taps = slice(first, min(first + PATCH_CALL, TAPS))
             nc.vector.quantize_mx(
-                out=patch_codes[:, tap, :].bitcast(FP8X4), scales=patch_scales[:, tap, :],
-                in_=patches[:, tap, :],
+                out=patch_codes[:, taps, :].rearrange(join).bitcast(FP8X4),
+                scales=patch_scales[:, taps, :].rearrange(join),
+                in_=patches[:, taps, :].rearrange(join),
             )
 
         weight_codes = keep.tile([P, TAPS, FILTERS], U32, align_bytes=64)
         weight_scales = keep.tile([P, TAPS, FILTERS], U8, align_bytes=64)
         acc = psum.tile([P, FILTERS], F32)
-        for tap in range(TAPS):
+        for first in range(0, TAPS, PAIR):
+            last = min(first + PAIR, TAPS)
             nc.vector.quantize_mx(
-                out=weight_codes[:, tap, :].bitcast(FP8X4), scales=weight_scales[:, tap, :],
-                in_=grouped[:, tap].rearrange("p f j -> p (f j)"),
+                out=weight_codes[:, first:last, :].rearrange(join).bitcast(FP8X4),
+                scales=weight_scales[:, first:last, :].rearrange(join),
+                in_=grouped[:, first:last].rearrange("p t f j -> p (t f j)"),
             )
-            nc.tensor.matmul_mx(
-                out=acc[:],
-                lhsT=patch_codes[:, tap, :].bitcast(FP8X4), lhsT_scale=patch_scales[:, tap, :],
-                rhs=weight_codes[:, tap, :].bitcast(FP8X4), rhs_scale=weight_scales[:, tap, :],
-                start=(tap == 0), stop=(tap == TAPS - 1),
-            )
+            for tap in range(first, last):
+                nc.tensor.matmul_mx(
+                    out=acc[:],
+                    lhsT=patch_codes[:, tap, :].bitcast(FP8X4), lhsT_scale=patch_scales[:, tap, :],
+                    rhs=weight_codes[:, tap, :].bitcast(FP8X4), rhs_scale=weight_scales[:, tap, :],
+                    start=(tap == 0), stop=(tap == TAPS - 1),
+                )
 
         result = keep.tile([ROWS, FILTERS], F32)
         nc.vector.tensor_tensor(out=result[:], in0=acc[0:ROWS, :], in1=addend[:], op=ALU.add)

@@ -23,8 +23,12 @@ POSITIONS = IMAGES * HEIGHT * WIDTH
 ROWS = IMAGES * OUT_SIDE * OUT_SIDE
 HALVES = 2
 PAIR = 2
-PATCH_CALL = 8
-STORE_SPLIT = 64
+IN_ROW = WIDTH * IMAGES
+OUT_ROW = OUT_SIDE * IMAGES
+BYTES = 4
+VERSIONS = 2
+BIAS_ROW = 96
+STORE_SPLIT = 32
 
 FLOPS = 2 * ROWS * TAPS * CHANNELS * 8 * FILTERS
 
@@ -39,7 +43,9 @@ def tile_conv2dkan_pa_s_kernel(
         stack.enter_context(tc.manual_schedule())
 
         x_sb = keep.tile([P, CHANNELS], BF16)
-        nc.scalar.dma_start(out=x_sb[:], in_=x.rearrange("b h w c -> (b h w) c"))
+        x_images = x.rearrange("b h w c -> b (h w) c")
+        for b in range(IMAGES):
+            nc.scalar.dma_start(out=x_sb[b:P:IMAGES, :], in_=x_images[b])
         factor = keep.tile([P, TAPS, FILTERS], BF16)
         factor_rows = scale_factor.rearrange("(t c) f -> c t f", t=TAPS)
         raw = keep.tile([P, TAPS, PACK, FILTERS], BF16)
@@ -62,21 +68,38 @@ def tile_conv2dkan_pa_s_kernel(
         for tap in range(1, TAPS):
             load_raw(tap)
 
-        ident = keep.tile([P, P], F32)
-        make_identity(nc, ident[:])
-        ones = keep.tile([P, P], BF16)
-        nc.gpsimd.memset(ones[:], 1.0)
-        bias_rows = keep.tile([P, FILTERS], BF16)
-        nc.vector.memset(bias_rows[:].bitcast(I32), 0)
-        nc.gpsimd.dma_start(out=bias_rows[0:1, :], in_=kan_bias.rearrange("(o f) -> o f", o=1))
-        nc.gpsimd.dma_start(out=bias_rows[1:2, :], in_=conv_bias.rearrange("(o f) -> o f", o=1))
-        base_sb = keep.tile([ROWS, FILTERS], BF16)
-        nc.gpsimd.dma_start(out=base_sb[:], in_=base.rearrange("b p q f -> (b p q) f"))
-        patches = keep.tile([P, TAPS, P * PACK], BF16, align_bytes=64)
-        nc.vector.memset(patches[:].bitcast(I32)[:, :, ROWS * PACK // 2 :], 0)
         warm = keep.tile([P, 1], F32)
         nc.vector.memset(warm[:], 0.0)
         nc.scalar.activation(out=warm[:], in_=warm[:], func=ACT.Abs)
+        ident = keep.tile([P, P], F32)
+        make_identity(nc, ident[:])
+        pick = keep.tile([P, P], BF16)
+        make_identity(nc, pick[:])
+        nc.gpsimd.memset(pick[BIAS_ROW : BIAS_ROW + 2, :], 1.0)
+        half_shift = keep.tile([P, HALVES], F32)
+        for h in range(HALVES):
+            nc.vector.memset(half_shift[:, h : h + 1], 3.5 - PACK * h)
+        added = keep.tile([P, FILTERS], BF16)
+        nc.vector.memset(added[:].bitcast(I32), 0)
+        base_images = base.rearrange("b p q f -> b (p q) f")
+        for b in range(IMAGES):
+            nc.gpsimd.dma_start(out=added[b:ROWS:IMAGES, :], in_=base_images[b])
+        nc.gpsimd.dma_start(
+            out=added[BIAS_ROW : BIAS_ROW + 1, :], in_=kan_bias.rearrange("(o f) -> o f", o=1)
+        )
+        nc.gpsimd.dma_start(
+            out=added[BIAS_ROW + 1 : BIAS_ROW + 2, :], in_=conv_bias.rearrange("(o f) -> o f", o=1)
+        )
+        both = keep.tile([P, VERSIONS, POSITIONS * PACK], BF16, align_bytes=64)
+        moved = (POSITIONS - IMAGES) * PACK
+        nc.vector.memset(both[:].bitcast(I32)[:, 1, moved // 2 :], 0)
+        both_codes = keep.tile([P, VERSIONS * POSITIONS], U32, align_bytes=64)
+        both_scales = keep.tile([P, VERSIONS * POSITIONS], U8, align_bytes=64)
+        nc.vector.memset(both_scales[:].bitcast(I32), 0)
+        patch_codes = keep.tile([P, TAPS, P], U32, align_bytes=64)
+        patch_scales = keep.tile([P, TAPS, P], U8, align_bytes=64)
+        nc.vector.memset(patch_codes[:].bitcast(I32)[:, :, ROWS:], 0)
+        nc.vector.memset(patch_scales[:].bitcast(I32)[:, :, ROWS // BYTES :], 0)
 
         weight = keep.tile([P, TAPS, PACK, FILTERS], BF16)
         grouped = keep.tile([P, TAPS, FILTERS, PACK], BF16, align_bytes=64)
@@ -95,12 +118,17 @@ def tile_conv2dkan_pa_s_kernel(
                 in_=weight[:, tap].rearrange("p j (c i) -> p c j i", i=4),
             )
 
+        def multiply_and_regroup_pair(first):
+            multiply(first, PAIR)
+            for tap in range(first, first + PAIR):
+                regroup(tap)
+
         centred = keep.tile([P, CHANNELS, HALVES], F32)
-        for h in range(HALVES):
-            nc.vector.tensor_scalar(
-                out=centred[:, :, h], in0=x_sb[:], scalar1=2.5, scalar2=3.5 - PACK * h,
-                op0=ALU.mult, op1=ALU.add,
-            )
+        nc.vector.scalar_tensor_tensor(
+            out=centred[:], in0=x_sb[:].unsqueeze(2).to_broadcast([P, CHANNELS, HALVES]), scalar=2.5,
+            in1=half_shift[:].unsqueeze(1).to_broadcast([P, CHANNELS, HALVES]),
+            op0=ALU.mult, op1=ALU.add,
+        )
         centred_t = psum.tile([P, POSITIONS], F32)
         nc.tensor.transpose(centred_t[:], centred[:].rearrange("p c h -> p (c h)"), ident[:])
         multiply(0, 1)
@@ -121,13 +149,8 @@ def tile_conv2dkan_pa_s_kernel(
         nc.vector.tensor_scalar(
             out=inner_neg[:], in0=dist[:], scalar1=1.0, scalar2=-1.0, op0=ALU.min, op1=ALU.add
         )
-
-        def multiply_and_regroup_pair(first):
-            multiply(first, PAIR)
-            for tap in range(first, first + PAIR):
-                regroup(tap)
-
         multiply_and_regroup_pair(1)
+
         flat = "p j n -> p (j n)"
         outer_term = keep.tile(planes, F32)
         nc.vector.scalar_tensor_tensor(
@@ -139,43 +162,46 @@ def tile_conv2dkan_pa_s_kernel(
             out=inner_term[:].rearrange(flat), in0=inner_sq[:].rearrange(flat), scalar=2.0 / 3.0,
             in1=inner_neg[:].rearrange(flat), op0=ALU.mult, op1=ALU.mult,
         )
-        basis = keep.tile([P, POSITIONS, PACK], BF16)
         nc.vector.tensor_tensor(
-            out=basis[:], in0=outer_term[:].rearrange("p j n -> p n j"),
+            out=both[:, 0, :].rearrange("p (n j) -> p n j", j=PACK),
+            in0=outer_term[:].rearrange("p j n -> p n j"),
             in1=inner_term[:].rearrange("p j n -> p n j"), op=ALU.add,
         )
-        for first in range(1 + PAIR, TAPS, PAIR):
-            multiply_and_regroup_pair(first)
-
-        bias_sum = psum.tile([P, FILTERS], F32)
-        nc.tensor.matmul(bias_sum[:], lhsT=ones[:], rhs=bias_rows[:], start=True, stop=True)
+        multiply_and_regroup_pair(1 + PAIR)
+        nc.vector.tensor_copy(out=both[:, 1, 0:moved], in_=both[:, 0, IMAGES * PACK :])
+        multiply_and_regroup_pair(1 + 2 * PAIR)
+        addend_ps = psum.tile([P, FILTERS], F32)
+        nc.tensor.matmul(addend_ps[:], lhsT=pick[:], rhs=added[:], start=True, stop=True)
         addend = keep.tile([ROWS, FILTERS], F32)
-        nc.vector.tensor_tensor(out=addend[:], in0=bias_sum[0:ROWS, :], in1=base_sb[:], op=ALU.add)
+        nc.scalar.copy(out=addend[:], in_=addend_ps[0:ROWS, :])
+        nc.vector.quantize_mx(
+            out=both_codes[:].bitcast(FP8X4), scales=both_scales[:],
+            in_=both[:].rearrange("p v e -> p (v e)"),
+        )
+        multiply_and_regroup_pair(1 + 3 * PAIR)
 
-        run = OUT_SIDE * PACK
-        basis_rows = basis[:].rearrange("p (b r s) j -> p b r (s j)", b=IMAGES, r=HEIGHT)
+        code_rows = both_codes[:].bitcast(I32).rearrange("p (v r c) -> p v r c", v=VERSIONS, r=HEIGHT)
+        scale_rows = both_scales[:].bitcast(I32).rearrange(
+            "p (v r c) -> p v r c", v=VERSIONS, r=HEIGHT
+        )
+        window_codes = patch_codes[:].bitcast(I32)
+        window_scales = patch_scales[:].bitcast(I32)
         for tap in range(TAPS):
             di, dj = divmod(tap, KERNEL)
+            version, step = dj % VERSIONS, dj // VERSIONS
             nc.vector.tensor_copy(
-                out=patches[:, tap, 0 : ROWS * PACK].rearrange(
-                    "p (b r sj) -> p b r sj", b=IMAGES, r=OUT_SIDE
-                ),
-                in_=basis_rows[:, :, di : di + OUT_SIDE, dj * PACK : dj * PACK + run],
+                out=window_codes[:, tap, 0:ROWS].rearrange("p (r c) -> p r c", r=OUT_SIDE),
+                in_=code_rows[:, version, di : di + OUT_SIDE, step * BYTES : step * BYTES + OUT_ROW],
             )
-        patch_codes = keep.tile([P, TAPS, P], U32, align_bytes=64)
-        patch_scales = keep.tile([P, TAPS, P], U8, align_bytes=64)
-        join = "p t e -> p (t e)"
-        for first in range(0, TAPS, PATCH_CALL):
-            taps = slice(first, min(first + PATCH_CALL, TAPS))
-            nc.vector.quantize_mx(
-                out=patch_codes[:, taps, :].rearrange(join).bitcast(FP8X4),
-                scales=patch_scales[:, taps, :].rearrange(join),
-                in_=patches[:, taps, :].rearrange(join),
+            nc.vector.tensor_copy(
+                out=window_scales[:, tap, 0 : ROWS // BYTES].rearrange("p (r c) -> p r c", r=OUT_SIDE),
+                in_=scale_rows[:, version, di : di + OUT_SIDE, step : step + OUT_ROW // BYTES],
             )
 
         weight_codes = keep.tile([P, TAPS, FILTERS], U32, align_bytes=64)
         weight_scales = keep.tile([P, TAPS, FILTERS], U8, align_bytes=64)
         acc = psum.tile([P, FILTERS], F32)
+        join = "p t e -> p (t e)"
         for first in range(0, TAPS, PAIR):
             last = min(first + PAIR, TAPS)
             nc.vector.quantize_mx(
@@ -193,6 +219,11 @@ def tile_conv2dkan_pa_s_kernel(
 
         result = keep.tile([ROWS, FILTERS], F32)
         nc.vector.tensor_tensor(out=result[:], in0=acc[0:ROWS, :], in1=addend[:], op=ALU.add)
-        out_rows = out.rearrange("b p q f -> (b p q) f")
-        nc.sync.dma_start(out=out_rows[0:STORE_SPLIT, :], in_=result[0:STORE_SPLIT, :])
-        nc.scalar.dma_start(out=out_rows[STORE_SPLIT:ROWS, :], in_=result[STORE_SPLIT:ROWS, :])
+        out_images = out.rearrange("b p q f -> b (p q) f")
+        cut = STORE_SPLIT * IMAGES
+        queues = [nc.sync, nc.scalar]
+        for b in range(IMAGES):
+            queues[b].dma_start(out=out_images[b, 0:STORE_SPLIT, :], in_=result[b:cut:IMAGES, :])
+            queues[b].dma_start(
+                out=out_images[b, STORE_SPLIT:, :], in_=result[cut + b : ROWS : IMAGES, :]
+            )

@@ -26,7 +26,6 @@ PAIR = 2
 IN_ROW = WIDTH * IMAGES
 OUT_ROW = OUT_SIDE * IMAGES
 BYTES = 4
-VERSIONS = 2
 BIAS_ROW = 96
 STORE_SPLIT = 32
 
@@ -90,12 +89,10 @@ def tile_conv2dkan_pa_s_kernel(
         nc.gpsimd.dma_start(
             out=added[BIAS_ROW + 1 : BIAS_ROW + 2, :], in_=conv_bias.rearrange("(o f) -> o f", o=1)
         )
-        both = keep.tile([P, VERSIONS, POSITIONS * PACK], BF16, align_bytes=64)
-        moved = (POSITIONS - IMAGES) * PACK
-        nc.vector.memset(both[:].bitcast(I32)[:, 1, moved // 2 :], 0)
-        both_codes = keep.tile([P, VERSIONS * POSITIONS], U32, align_bytes=64)
-        both_scales = keep.tile([P, VERSIONS * POSITIONS], U8, align_bytes=64)
-        nc.vector.memset(both_scales[:].bitcast(I32), 0)
+        basis = keep.tile([P, POSITIONS * PACK], BF16, align_bytes=64)
+        basis_codes = keep.tile([P, POSITIONS], U32, align_bytes=64)
+        basis_scales = keep.tile([P, POSITIONS], U8, align_bytes=64)
+        nc.vector.memset(basis_scales[:].bitcast(I32), 0)
         patch_codes = keep.tile([P, TAPS, P], U32, align_bytes=64)
         patch_scales = keep.tile([P, TAPS, P], U8, align_bytes=64)
         nc.vector.memset(patch_codes[:].bitcast(I32)[:, :, ROWS:], 0)
@@ -116,6 +113,13 @@ def tile_conv2dkan_pa_s_kernel(
             nc.scalar.copy(
                 out=grouped[:, tap].rearrange("p (c i) j -> p c j i", i=4),
                 in_=weight[:, tap].rearrange("p j (c i) -> p c j i", i=4),
+            )
+
+        def multiply_grouped(tap):
+            nc.vector.tensor_tensor(
+                out=grouped[:, tap], in0=raw[:, tap].rearrange("p j f -> p f j"),
+                in1=factor[:, tap, :].unsqueeze(2).to_broadcast([P, FILTERS, PACK]),
+                op=ALU.mult,
             )
 
         def multiply_and_regroup_pair(first):
@@ -163,47 +167,64 @@ def tile_conv2dkan_pa_s_kernel(
             in1=inner_neg[:].rearrange(flat), op0=ALU.mult, op1=ALU.mult,
         )
         nc.vector.tensor_tensor(
-            out=both[:, 0, :].rearrange("p (n j) -> p n j", j=PACK),
+            out=basis[:].rearrange("p (n j) -> p n j", j=PACK),
             in0=outer_term[:].rearrange("p j n -> p n j"),
             in1=inner_term[:].rearrange("p j n -> p n j"), op=ALU.add,
         )
         multiply_and_regroup_pair(1 + PAIR)
-        nc.vector.tensor_copy(out=both[:, 1, 0:moved], in_=both[:, 0, IMAGES * PACK :])
         multiply_and_regroup_pair(1 + 2 * PAIR)
         addend_ps = psum.tile([P, FILTERS], F32)
         nc.tensor.matmul(addend_ps[:], lhsT=pick[:], rhs=added[:], start=True, stop=True)
         addend = keep.tile([ROWS, FILTERS], F32)
         nc.scalar.copy(out=addend[:], in_=addend_ps[0:ROWS, :])
         nc.vector.quantize_mx(
-            out=both_codes[:].bitcast(FP8X4), scales=both_scales[:],
-            in_=both[:].rearrange("p v e -> p (v e)"),
+            out=basis_codes[:].bitcast(FP8X4), scales=basis_scales[:], in_=basis[:]
         )
-        multiply_and_regroup_pair(1 + 3 * PAIR)
+        multiply(1 + 3 * PAIR, 1)
+        regroup(1 + 3 * PAIR)
 
-        code_rows = both_codes[:].bitcast(I32).rearrange("p (v r c) -> p v r c", v=VERSIONS, r=HEIGHT)
-        scale_rows = both_scales[:].bitcast(I32).rearrange(
-            "p (v r c) -> p v r c", v=VERSIONS, r=HEIGHT
-        )
         window_codes = patch_codes[:].bitcast(I32)
         window_scales = patch_scales[:].bitcast(I32)
-        for tap in range(TAPS):
-            di, dj = divmod(tap, KERNEL)
-            version, step = dj % VERSIONS, dj // VERSIONS
+        by_row = "p (r c) -> p r c"
+        code_rows = basis_codes[:].bitcast(I32).rearrange(by_row, r=HEIGHT)
+        scale_rows = basis_scales[:].rearrange(by_row, r=HEIGHT)
+        scale_word_rows = basis_scales[:].bitcast(I32).rearrange(by_row, r=HEIGHT)
+        narrow = HEIGHT * OUT_ROW
+        for dj in range(KERNEL):
+            shift = dj * IMAGES
             nc.vector.tensor_copy(
-                out=window_codes[:, tap, 0:ROWS].rearrange("p (r c) -> p r c", r=OUT_SIDE),
-                in_=code_rows[:, version, di : di + OUT_SIDE, step * BYTES : step * BYTES + OUT_ROW],
+                out=window_codes[:, dj, 0:narrow].rearrange(by_row, r=HEIGHT),
+                in_=code_rows[:, :, shift : shift + OUT_ROW],
+            )
+            if shift % BYTES == 0:
+                nc.vector.tensor_copy(
+                    out=window_scales[:, dj, 0 : narrow // BYTES].rearrange(by_row, r=HEIGHT),
+                    in_=scale_word_rows[:, :, shift // BYTES : (shift + OUT_ROW) // BYTES],
+                )
+            else:
+                nc.vector.tensor_copy(
+                    out=patch_scales[:, dj, 0:narrow].rearrange(by_row, r=HEIGHT),
+                    in_=scale_rows[:, :, shift : shift + OUT_ROW],
+                )
+        multiply_grouped(TAPS - 1)
+        for di in range(1, KERNEL):
+            taps = slice(di * KERNEL, (di + 1) * KERNEL)
+            start = di * OUT_ROW
+            nc.vector.tensor_copy(
+                out=window_codes[:, taps, 0:ROWS], in_=window_codes[:, 0:KERNEL, start : start + ROWS]
             )
             nc.vector.tensor_copy(
-                out=window_scales[:, tap, 0 : ROWS // BYTES].rearrange("p (r c) -> p r c", r=OUT_SIDE),
-                in_=scale_rows[:, version, di : di + OUT_SIDE, step : step + OUT_ROW // BYTES],
+                out=window_scales[:, taps, 0 : ROWS // BYTES],
+                in_=window_scales[:, 0:KERNEL, start // BYTES : (start + ROWS) // BYTES],
             )
 
         weight_codes = keep.tile([P, TAPS, FILTERS], U32, align_bytes=64)
         weight_scales = keep.tile([P, TAPS, FILTERS], U8, align_bytes=64)
         acc = psum.tile([P, FILTERS], F32)
         join = "p t e -> p (t e)"
-        for first in range(0, TAPS, PAIR):
-            last = min(first + PAIR, TAPS)
+        groups = [(0, 2), (2, 4), (4, 6), (8, 9), (6, 7), (7, 8)]
+        done = 0
+        for first, last in groups:
             nc.vector.quantize_mx(
                 out=weight_codes[:, first:last, :].rearrange(join).bitcast(FP8X4),
                 scales=weight_scales[:, first:last, :].rearrange(join),
@@ -214,8 +235,9 @@ def tile_conv2dkan_pa_s_kernel(
                     out=acc[:],
                     lhsT=patch_codes[:, tap, :].bitcast(FP8X4), lhsT_scale=patch_scales[:, tap, :],
                     rhs=weight_codes[:, tap, :].bitcast(FP8X4), rhs_scale=weight_scales[:, tap, :],
-                    start=(tap == 0), stop=(tap == TAPS - 1),
+                    start=(done == 0), stop=(done == TAPS - 1),
                 )
+                done += 1
 
         result = keep.tile([ROWS, FILTERS], F32)
         nc.vector.tensor_tensor(out=result[:], in0=acc[0:ROWS, :], in1=addend[:], op=ALU.add)

@@ -61,11 +61,10 @@ def tile_conv2dkan_pa_s_kernel(
                 out=raw[:, tap], in_=raw_rows[tap].rearrange("(p j) f -> p j f", j=PACK)
             )
 
-        load_factor(0, 1)
-        load_raw(0)
-        load_factor(1, TAPS)
-        for tap in range(1, TAPS):
-            load_raw(tap)
+        for first, last in [(0, 1), (1, 2), (2, 4), (4, 6), (6, TAPS)]:
+            load_factor(first, last)
+            for tap in range(first, last):
+                load_raw(tap)
 
         warm = keep.tile([P, 1], F32)
         nc.vector.memset(warm[:], 0.0)
@@ -96,7 +95,7 @@ def tile_conv2dkan_pa_s_kernel(
         patch_codes = keep.tile([P, TAPS, P], U32, align_bytes=64)
         patch_scales = keep.tile([P, TAPS, P], U8, align_bytes=64)
         nc.vector.memset(patch_codes[:].bitcast(I32)[:, :, ROWS:], 0)
-        nc.vector.memset(patch_scales[:].bitcast(I32)[:, :, ROWS // BYTES :], 0)
+        nc.vector.memset(patch_scales[:].bitcast(I32), 0)
 
         weight = keep.tile([P, TAPS, PACK, FILTERS], BF16)
         grouped = keep.tile([P, TAPS, FILTERS, PACK], BF16, align_bytes=64)
@@ -136,6 +135,7 @@ def tile_conv2dkan_pa_s_kernel(
         centred_t = psum.tile([P, POSITIONS], F32)
         nc.tensor.transpose(centred_t[:], centred[:].rearrange("p c h -> p (c h)"), ident[:])
         multiply(0, 1)
+        multiply(1, 1)
         planes = [P, PACK, POSITIONS]
         dist = keep.tile(planes, F32)
         for j in range(PACK):
@@ -145,6 +145,7 @@ def tile_conv2dkan_pa_s_kernel(
         inner_sq = keep.tile(planes, F32)
         nc.scalar.activation(out=inner_sq[:], in_=dist[:], func=ACT.Square, bias=1.0, scale=-1.0)
         regroup(0)
+        regroup(1)
         outer_neg = keep.tile(planes, F32)
         nc.vector.tensor_scalar(
             out=outer_neg[:], in0=dist[:], scalar1=2.0, scalar2=-2.0, op0=ALU.min, op1=ALU.add
@@ -153,7 +154,7 @@ def tile_conv2dkan_pa_s_kernel(
         nc.vector.tensor_scalar(
             out=inner_neg[:], in0=dist[:], scalar1=1.0, scalar2=-1.0, op0=ALU.min, op1=ALU.add
         )
-        multiply_and_regroup_pair(1)
+        multiply_and_regroup_pair(2)
 
         flat = "p j n -> p (j n)"
         outer_term = keep.tile(planes, F32)
@@ -171,17 +172,14 @@ def tile_conv2dkan_pa_s_kernel(
             in0=outer_term[:].rearrange("p j n -> p n j"),
             in1=inner_term[:].rearrange("p j n -> p n j"), op=ALU.add,
         )
-        multiply_and_regroup_pair(1 + PAIR)
-        multiply_and_regroup_pair(1 + 2 * PAIR)
+        multiply_and_regroup_pair(2 + PAIR)
+        nc.vector.quantize_mx(
+            out=basis_codes[:].bitcast(FP8X4), scales=basis_scales[:], in_=basis[:]
+        )
         addend_ps = psum.tile([P, FILTERS], F32)
         nc.tensor.matmul(addend_ps[:], lhsT=pick[:], rhs=added[:], start=True, stop=True)
         addend = keep.tile([ROWS, FILTERS], F32)
         nc.scalar.copy(out=addend[:], in_=addend_ps[0:ROWS, :])
-        nc.vector.quantize_mx(
-            out=basis_codes[:].bitcast(FP8X4), scales=basis_scales[:], in_=basis[:]
-        )
-        multiply(1 + 3 * PAIR, 1)
-        regroup(1 + 3 * PAIR)
 
         window_codes = patch_codes[:].bitcast(I32)
         window_scales = patch_scales[:].bitcast(I32)
@@ -206,17 +204,18 @@ def tile_conv2dkan_pa_s_kernel(
                     out=patch_scales[:, dj, 0:narrow].rearrange(by_row, r=HEIGHT),
                     in_=scale_rows[:, :, shift : shift + OUT_ROW],
                 )
-        multiply_grouped(TAPS - 1)
         for di in range(1, KERNEL):
             taps = slice(di * KERNEL, (di + 1) * KERNEL)
             start = di * OUT_ROW
-            nc.vector.tensor_copy(
+            nc.sync.dma_start(
                 out=window_codes[:, taps, 0:ROWS], in_=window_codes[:, 0:KERNEL, start : start + ROWS]
             )
-            nc.vector.tensor_copy(
+            nc.sync.dma_start(
                 out=window_scales[:, taps, 0 : ROWS // BYTES],
                 in_=window_scales[:, 0:KERNEL, start // BYTES : (start + ROWS) // BYTES],
             )
+        multiply_and_regroup_pair(2 + 2 * PAIR)
+        multiply_grouped(TAPS - 1)
 
         weight_codes = keep.tile([P, TAPS, FILTERS], U32, align_bytes=64)
         weight_scales = keep.tile([P, TAPS, FILTERS], U8, align_bytes=64)

@@ -48,7 +48,9 @@ def tile_conv2dkan_pa_s_kernel(
         factor = keep.tile([P, TAPS, FILTERS], BF16)
         factor_rows = scale_factor.rearrange("(t c) f -> c t f", t=TAPS)
         raw = keep.tile([P, TAPS, PACK, FILTERS], BF16)
-        raw_rows = spline_kernel.rearrange("(t c) k f -> t (c k) f", t=TAPS)
+        raw_rows = spline_kernel.rearrange("(t c) k f -> t (c k) f", t=TAPS).rearrange(
+            "t (p j) f -> p t (j f)", j=PACK
+        )
 
         def load_factor(first, last):
             for h in range(HALVES):
@@ -56,15 +58,15 @@ def tile_conv2dkan_pa_s_kernel(
                     out=factor[h:P:HALVES, first:last, :], in_=factor_rows[:, first:last, :]
                 )
 
-        def load_raw(tap):
+        def load_raw(first, last):
             nc.sync.dma_start(
-                out=raw[:, tap], in_=raw_rows[tap].rearrange("(p j) f -> p j f", j=PACK)
+                out=raw[:, first:last].rearrange("p t j f -> p t (j f)"),
+                in_=raw_rows[:, first:last, :],
             )
 
         for first, last in [(0, 1), (1, 2), (2, 4), (4, 6), (6, TAPS)]:
             load_factor(first, last)
-            for tap in range(first, last):
-                load_raw(tap)
+            load_raw(first, last)
 
         warm = keep.tile([P, 1], F32)
         nc.vector.memset(warm[:], 0.0)
@@ -114,12 +116,8 @@ def tile_conv2dkan_pa_s_kernel(
                 in_=weight[:, tap].rearrange("p j (c i) -> p c j i", i=4),
             )
 
-        def multiply_grouped(tap):
-            nc.vector.tensor_tensor(
-                out=grouped[:, tap], in0=raw[:, tap].rearrange("p j f -> p f j"),
-                in1=factor[:, tap, :].unsqueeze(2).to_broadcast([P, FILTERS, PACK]),
-                op=ALU.mult,
-            )
+        def regroup_on_vector(tap):
+            nc.vector.tensor_copy(out=grouped[:, tap], in_=weight[:, tap].rearrange("p j f -> p f j"))
 
         def multiply_and_regroup_pair(first):
             multiply(first, PAIR)
@@ -214,8 +212,9 @@ def tile_conv2dkan_pa_s_kernel(
                 out=window_scales[:, taps, 0 : ROWS // BYTES],
                 in_=window_scales[:, 0:KERNEL, start // BYTES : (start + ROWS) // BYTES],
             )
-        multiply_and_regroup_pair(2 + 2 * PAIR)
-        multiply_grouped(TAPS - 1)
+        multiply(2 + 2 * PAIR, PAIR + 1)
+        for tap in range(2 + 2 * PAIR, TAPS - 1):
+            regroup(tap)
 
         weight_codes = keep.tile([P, TAPS, FILTERS], U32, align_bytes=64)
         weight_scales = keep.tile([P, TAPS, FILTERS], U8, align_bytes=64)
@@ -224,6 +223,8 @@ def tile_conv2dkan_pa_s_kernel(
         groups = [(0, 2), (2, 4), (4, 6), (8, 9), (6, 7), (7, 8)]
         done = 0
         for first, last in groups:
+            if first == 2:
+                regroup_on_vector(TAPS - 1)
             nc.vector.quantize_mx(
                 out=weight_codes[:, first:last, :].rearrange(join).bitcast(FP8X4),
                 scales=weight_scales[:, first:last, :].rearrange(join),

@@ -138,37 +138,38 @@ def tile_conv2dkan_pa_s_kernel(
         dist = keep.tile(planes, F32)
         for j in range(PACK):
             nc.scalar.activation(out=dist[:, j, :], in_=centred_t[:], func=ACT.Abs, bias=-float(j))
-        outer_sq = keep.tile(planes, F32)
-        nc.scalar.activation(out=outer_sq[:], in_=dist[:], func=ACT.Square, bias=2.0, scale=-1.0)
-        inner_sq = keep.tile(planes, F32)
-        nc.scalar.activation(out=inner_sq[:], in_=dist[:], func=ACT.Square, bias=1.0, scale=-1.0)
+        packed = [P, POSITIONS, PACK]
+        dist_packed = dist[:].rearrange("p j n -> p n j")
+        outer_sq = keep.tile(packed, F32)
+        nc.scalar.activation(out=outer_sq[:], in_=dist_packed, func=ACT.Square, bias=2.0, scale=-1.0)
+        inner_sq = keep.tile(packed, F32)
+        nc.scalar.activation(out=inner_sq[:], in_=dist_packed, func=ACT.Square, bias=1.0, scale=-1.0)
         regroup(0)
         regroup(1)
-        outer_neg = keep.tile(planes, F32)
+        outer_neg = keep.tile(packed, F32)
         nc.vector.tensor_scalar(
-            out=outer_neg[:], in0=dist[:], scalar1=2.0, scalar2=-2.0, op0=ALU.min, op1=ALU.add
+            out=outer_neg[:], in0=dist_packed, scalar1=2.0, scalar2=-2.0, op0=ALU.min, op1=ALU.add
         )
-        inner_neg = keep.tile(planes, F32)
+        inner_neg = keep.tile(packed, F32)
         nc.vector.tensor_scalar(
-            out=inner_neg[:], in0=dist[:], scalar1=1.0, scalar2=-1.0, op0=ALU.min, op1=ALU.add
+            out=inner_neg[:], in0=dist_packed, scalar1=1.0, scalar2=-1.0, op0=ALU.min, op1=ALU.add
         )
         multiply_and_regroup_pair(2)
 
-        flat = "p j n -> p (j n)"
-        outer_term = keep.tile(planes, F32)
+        flat = "p n j -> p (n j)"
+        outer_term = keep.tile(packed, F32)
         nc.vector.scalar_tensor_tensor(
             out=outer_term[:].rearrange(flat), in0=outer_sq[:].rearrange(flat), scalar=-1.0 / 6.0,
             in1=outer_neg[:].rearrange(flat), op0=ALU.mult, op1=ALU.mult,
         )
-        inner_term = keep.tile(planes, F32)
+        inner_term = keep.tile(packed, F32)
         nc.vector.scalar_tensor_tensor(
             out=inner_term[:].rearrange(flat), in0=inner_sq[:].rearrange(flat), scalar=2.0 / 3.0,
             in1=inner_neg[:].rearrange(flat), op0=ALU.mult, op1=ALU.mult,
         )
         nc.vector.tensor_tensor(
-            out=basis[:].rearrange("p (n j) -> p n j", j=PACK),
-            in0=outer_term[:].rearrange("p j n -> p n j"),
-            in1=inner_term[:].rearrange("p j n -> p n j"), op=ALU.add,
+            out=basis[:], in0=outer_term[:].rearrange(flat), in1=inner_term[:].rearrange(flat),
+            op=ALU.add,
         )
         multiply_and_regroup_pair(2 + PAIR)
         nc.vector.quantize_mx(

@@ -19,6 +19,7 @@ KERNEL = 3
 TAPS = KERNEL * KERNEL
 OUT_SIDE = HEIGHT - KERNEL + 1
 FILTERS = 256
+HALF_FILTERS = FILTERS // 2
 POSITIONS = IMAGES * HEIGHT * WIDTH
 ROWS = IMAGES * OUT_SIDE * OUT_SIDE
 HALVES = 2
@@ -83,11 +84,11 @@ def tile_conv2dkan_pa_s_kernel(
         nc.vector.memset(added[:].bitcast(I32), 0)
         base_images = base.rearrange("b p q f -> b (p q) f")
         for b in range(IMAGES):
-            nc.gpsimd.dma_start(out=added[b:ROWS:IMAGES, :], in_=base_images[b])
-        nc.gpsimd.dma_start(
+            nc.sync.dma_start(out=added[b:ROWS:IMAGES, :], in_=base_images[b])
+        nc.sync.dma_start(
             out=added[BIAS_ROW : BIAS_ROW + 1, :], in_=kan_bias.rearrange("(o f) -> o f", o=1)
         )
-        nc.gpsimd.dma_start(
+        nc.sync.dma_start(
             out=added[BIAS_ROW + 1 : BIAS_ROW + 2, :], in_=conv_bias.rearrange("(o f) -> o f", o=1)
         )
         basis = keep.tile([P, POSITIONS * PACK], BF16, align_bytes=64)
@@ -110,10 +111,10 @@ def tile_conv2dkan_pa_s_kernel(
                 op=ALU.mult,
             )
 
-        def regroup(tap):
+        def regroup(tap, columns=slice(0, FILTERS)):
             nc.scalar.copy(
-                out=grouped[:, tap].rearrange("p (c i) j -> p c j i", i=4),
-                in_=weight[:, tap].rearrange("p j (c i) -> p c j i", i=4),
+                out=grouped[:, tap, columns].rearrange("p (c i) j -> p c j i", i=4),
+                in_=weight[:, tap, :, columns].rearrange("p j (c i) -> p c j i", i=4),
             )
 
         def regroup_on_vector(tap):
@@ -124,61 +125,79 @@ def tile_conv2dkan_pa_s_kernel(
             for tap in range(first, first + PAIR):
                 regroup(tap)
 
+        weight_codes = keep.tile([P, TAPS, FILTERS], U32, align_bytes=64)
+        weight_scales = keep.tile([P, TAPS, FILTERS], U8, align_bytes=64)
+        join = "p t e -> p (t e)"
+
+        def quantize(first, last, columns):
+            nc.vector.quantize_mx(
+                out=weight_codes[:, first:last, columns].rearrange(join).bitcast(FP8X4),
+                scales=weight_scales[:, first:last, columns].rearrange(join),
+                in_=grouped[:, first:last, columns].rearrange("p t f j -> p (t f j)"),
+            )
+
         centred = keep.tile([P, CHANNELS, HALVES], F32)
         nc.vector.scalar_tensor_tensor(
             out=centred[:], in0=x_sb[:].unsqueeze(2).to_broadcast([P, CHANNELS, HALVES]), scalar=2.5,
             in1=half_shift[:].unsqueeze(1).to_broadcast([P, CHANNELS, HALVES]),
             op0=ALU.mult, op1=ALU.add,
         )
-        centred_t = psum.tile([P, POSITIONS], F32)
-        nc.tensor.transpose(centred_t[:], centred[:].rearrange("p c h -> p (c h)"), ident[:])
-        multiply(0, 1)
-        multiply(1, 1)
-        planes = [P, PACK, POSITIONS]
+        planes = [P, PACK, P]
+        flat = "p j m -> p (j m)"
         dist = keep.tile(planes, F32)
         for j in range(PACK):
-            nc.scalar.activation(out=dist[:, j, :], in_=centred_t[:], func=ACT.Abs, bias=-float(j))
-        packed = [P, POSITIONS, PACK]
-        dist_packed = dist[:].rearrange("p j n -> p n j")
-        outer_sq = keep.tile(packed, F32)
-        nc.scalar.activation(out=outer_sq[:], in_=dist_packed, func=ACT.Square, bias=2.0, scale=-1.0)
-        inner_sq = keep.tile(packed, F32)
-        nc.scalar.activation(out=inner_sq[:], in_=dist_packed, func=ACT.Square, bias=1.0, scale=-1.0)
-        regroup(0)
-        regroup(1)
-        outer_neg = keep.tile(packed, F32)
+            nc.scalar.activation(
+                out=dist[:, j, :], in_=centred[:].rearrange("p c h -> p (c h)"), func=ACT.Abs,
+                bias=-float(j),
+            )
+        outer_sq = keep.tile(planes, F32)
+        nc.scalar.activation(out=outer_sq[:], in_=dist[:], func=ACT.Square, bias=2.0, scale=-1.0)
+        inner_sq = keep.tile(planes, F32)
+        nc.scalar.activation(out=inner_sq[:], in_=dist[:], func=ACT.Square, bias=1.0, scale=-1.0)
+        multiply(0, 1)
+        outer_neg = keep.tile(planes, F32)
         nc.vector.tensor_scalar(
-            out=outer_neg[:], in0=dist_packed, scalar1=2.0, scalar2=-2.0, op0=ALU.min, op1=ALU.add
+            out=outer_neg[:], in0=dist[:], scalar1=2.0, scalar2=-2.0, op0=ALU.min, op1=ALU.add
         )
-        inner_neg = keep.tile(packed, F32)
+        inner_neg = keep.tile(planes, F32)
         nc.vector.tensor_scalar(
-            out=inner_neg[:], in0=dist_packed, scalar1=1.0, scalar2=-1.0, op0=ALU.min, op1=ALU.add
+            out=inner_neg[:], in0=dist[:], scalar1=1.0, scalar2=-1.0, op0=ALU.min, op1=ALU.add
         )
-        multiply_and_regroup_pair(2)
-
-        flat = "p n j -> p (n j)"
-        outer_term = keep.tile(packed, F32)
+        multiply(1, 1)
+        outer_term = keep.tile(planes, F32)
         nc.vector.scalar_tensor_tensor(
             out=outer_term[:].rearrange(flat), in0=outer_sq[:].rearrange(flat), scalar=-1.0 / 6.0,
             in1=outer_neg[:].rearrange(flat), op0=ALU.mult, op1=ALU.mult,
         )
-        inner_term = keep.tile(packed, F32)
+        inner_term = keep.tile(planes, F32)
         nc.vector.scalar_tensor_tensor(
             out=inner_term[:].rearrange(flat), in0=inner_sq[:].rearrange(flat), scalar=2.0 / 3.0,
             in1=inner_neg[:].rearrange(flat), op0=ALU.mult, op1=ALU.mult,
         )
-        nc.vector.tensor_tensor(
-            out=basis[:], in0=outer_term[:].rearrange(flat), in1=inner_term[:].rearrange(flat),
-            op=ALU.add,
-        )
+        basis_ps = psum.tile([P, PACK, POSITIONS], F32)
+        for term in (outer_term, inner_term):
+            for j in range(PACK):
+                nc.tensor.matmul(
+                    basis_ps[:, j, :], lhsT=term[:, j, :], rhs=ident[:], is_transpose=True,
+                    start=(term is outer_term and j == 0),
+                    stop=(term is inner_term and j == PACK - 1),
+                )
+        multiply(2, PAIR)
+        regroup(0)
+        regroup(1)
+        regroup(2)
+        regroup(3)
         multiply_and_regroup_pair(2 + PAIR)
+        nc.vector.tensor_copy(
+            out=basis[:].rearrange("p (n j) -> p n j", j=PACK),
+            in_=basis_ps[:].rearrange("p j n -> p n j"),
+        )
+        quantize(0, 2, slice(0, FILTERS))
         nc.vector.quantize_mx(
             out=basis_codes[:].bitcast(FP8X4), scales=basis_scales[:], in_=basis[:]
         )
         addend_ps = psum.tile([P, FILTERS], F32)
         nc.tensor.matmul(addend_ps[:], lhsT=pick[:], rhs=added[:], start=True, stop=True)
-        addend = keep.tile([ROWS, FILTERS], F32)
-        nc.scalar.copy(out=addend[:], in_=addend_ps[0:ROWS, :])
 
         window_codes = patch_codes[:].bitcast(I32)
         window_scales = patch_scales[:].bitcast(I32)
@@ -214,39 +233,52 @@ def tile_conv2dkan_pa_s_kernel(
                 in_=window_scales[:, 0:KERNEL, start // BYTES : (start + ROWS) // BYTES],
             )
         multiply(2 + 2 * PAIR, PAIR + 1)
-        for tap in range(2 + 2 * PAIR, TAPS - 1):
-            regroup(tap)
+        last_tap = TAPS - 2
+        halves = [slice(0, HALF_FILTERS), slice(HALF_FILTERS, FILTERS)]
+        regroup(last_tap - 1)
+        for columns in halves:
+            regroup(last_tap, columns)
+        addend = keep.tile([ROWS, FILTERS], F32)
+        nc.scalar.copy(out=addend[:], in_=addend_ps[0:ROWS, :])
 
-        weight_codes = keep.tile([P, TAPS, FILTERS], U32, align_bytes=64)
-        weight_scales = keep.tile([P, TAPS, FILTERS], U8, align_bytes=64)
-        acc = psum.tile([P, FILTERS], F32)
-        join = "p t e -> p (t e)"
-        groups = [(0, 2), (2, 4), (4, 6), (8, 9), (6, 7), (7, 8)]
-        done = 0
-        for first, last in groups:
-            if first == 2:
-                regroup_on_vector(TAPS - 1)
-            nc.vector.quantize_mx(
-                out=weight_codes[:, first:last, :].rearrange(join).bitcast(FP8X4),
-                scales=weight_scales[:, first:last, :].rearrange(join),
-                in_=grouped[:, first:last].rearrange("p t f j -> p (t f j)"),
+        acc_0 = psum.tile([P, HALF_FILTERS], F32)
+        acc_1 = psum.tile([P, HALF_FILTERS], F32)
+        accs = [acc_0, acc_1]
+        def multiply_accumulate(tap, half):
+            nc.tensor.matmul_mx(
+                out=accs[half][:],
+                lhsT=patch_codes[:, tap, :].bitcast(FP8X4), lhsT_scale=patch_scales[:, tap, :],
+                rhs=weight_codes[:, tap, halves[half]].bitcast(FP8X4),
+                rhs_scale=weight_scales[:, tap, halves[half]],
+                start=(tap == 0), stop=(tap == last_tap),
             )
+
+        for first, last in [(0, 2), (2, 4), (4, 6), (8, 9), (6, 7)]:
+            if first == 4:
+                regroup_on_vector(TAPS - 1)
+            if first > 0:
+                quantize(first, last, slice(0, FILTERS))
             for tap in range(first, last):
-                nc.tensor.matmul_mx(
-                    out=acc[:],
-                    lhsT=patch_codes[:, tap, :].bitcast(FP8X4), lhsT_scale=patch_scales[:, tap, :],
-                    rhs=weight_codes[:, tap, :].bitcast(FP8X4), rhs_scale=weight_scales[:, tap, :],
-                    start=(done == 0), stop=(done == TAPS - 1),
-                )
-                done += 1
+                for half in range(2):
+                    multiply_accumulate(tap, half)
+        for half in range(2):
+            quantize(last_tap, last_tap + 1, halves[half])
+            multiply_accumulate(last_tap, half)
 
         result = keep.tile([ROWS, FILTERS], F32)
-        nc.vector.tensor_tensor(out=result[:], in0=acc[0:ROWS, :], in1=addend[:], op=ALU.add)
         out_images = out.rearrange("b p q f -> b (p q) f")
         cut = STORE_SPLIT * IMAGES
         queues = [nc.sync, nc.scalar]
-        for b in range(IMAGES):
-            queues[b].dma_start(out=out_images[b, 0:STORE_SPLIT, :], in_=result[b:cut:IMAGES, :])
-            queues[b].dma_start(
-                out=out_images[b, STORE_SPLIT:, :], in_=result[cut + b : ROWS : IMAGES, :]
+        for half in range(2):
+            columns = halves[half]
+            nc.vector.tensor_tensor(
+                out=result[:, columns], in0=accs[half][0:ROWS, :], in1=addend[:, columns], op=ALU.add
             )
+            for b in range(IMAGES):
+                queues[b].dma_start(
+                    out=out_images[b, 0:STORE_SPLIT, columns], in_=result[b:cut:IMAGES, columns]
+                )
+                queues[b].dma_start(
+                    out=out_images[b, STORE_SPLIT:, columns],
+                    in_=result[cut + b : ROWS : IMAGES, columns],
+                )

@@ -19,7 +19,6 @@ KERNEL = 3
 TAPS = KERNEL * KERNEL
 OUT_SIDE = HEIGHT - KERNEL + 1
 FILTERS = 256
-HALF_FILTERS = FILTERS // 2
 POSITIONS = IMAGES * HEIGHT * WIDTH
 ROWS = IMAGES * OUT_SIDE * OUT_SIDE
 HALVES = 2
@@ -84,11 +83,11 @@ def tile_conv2dkan_pa_s_kernel(
         nc.vector.memset(added[:].bitcast(I32), 0)
         base_images = base.rearrange("b p q f -> b (p q) f")
         for b in range(IMAGES):
-            nc.sync.dma_start(out=added[b:ROWS:IMAGES, :], in_=base_images[b])
-        nc.sync.dma_start(
+            nc.gpsimd.dma_start(out=added[b:ROWS:IMAGES, :], in_=base_images[b])
+        nc.gpsimd.dma_start(
             out=added[BIAS_ROW : BIAS_ROW + 1, :], in_=kan_bias.rearrange("(o f) -> o f", o=1)
         )
-        nc.sync.dma_start(
+        nc.gpsimd.dma_start(
             out=added[BIAS_ROW + 1 : BIAS_ROW + 2, :], in_=conv_bias.rearrange("(o f) -> o f", o=1)
         )
         basis = keep.tile([P, POSITIONS * PACK], BF16, align_bytes=64)
@@ -111,10 +110,10 @@ def tile_conv2dkan_pa_s_kernel(
                 op=ALU.mult,
             )
 
-        def regroup(tap, columns=slice(0, FILTERS)):
+        def regroup(tap):
             nc.scalar.copy(
-                out=grouped[:, tap, columns].rearrange("p (c i) j -> p c j i", i=4),
-                in_=weight[:, tap, :, columns].rearrange("p j (c i) -> p c j i", i=4),
+                out=grouped[:, tap].rearrange("p (c i) j -> p c j i", i=4),
+                in_=weight[:, tap].rearrange("p j (c i) -> p c j i", i=4),
             )
 
         def regroup_on_vector(tap):
@@ -129,11 +128,11 @@ def tile_conv2dkan_pa_s_kernel(
         weight_scales = keep.tile([P, TAPS, FILTERS], U8, align_bytes=64)
         join = "p t e -> p (t e)"
 
-        def quantize(first, last, columns):
+        def quantize(first, last):
             nc.vector.quantize_mx(
-                out=weight_codes[:, first:last, columns].rearrange(join).bitcast(FP8X4),
-                scales=weight_scales[:, first:last, columns].rearrange(join),
-                in_=grouped[:, first:last, columns].rearrange("p t f j -> p (t f j)"),
+                out=weight_codes[:, first:last, :].rearrange(join).bitcast(FP8X4),
+                scales=weight_scales[:, first:last, :].rearrange(join),
+                in_=grouped[:, first:last].rearrange("p t f j -> p (t f j)"),
             )
 
         centred = keep.tile([P, CHANNELS, HALVES], F32)
@@ -192,13 +191,10 @@ def tile_conv2dkan_pa_s_kernel(
             out=basis[:].rearrange("p (n j) -> p n j", j=PACK),
             in_=basis_ps[:].rearrange("p j n -> p n j"),
         )
-        quantize(0, 2, slice(0, FILTERS))
+        quantize(0, 2)
         nc.vector.quantize_mx(
             out=basis_codes[:].bitcast(FP8X4), scales=basis_scales[:], in_=basis[:]
         )
-        addend_ps = psum.tile([P, FILTERS], F32)
-        nc.tensor.matmul(addend_ps[:], lhsT=pick[:], rhs=added[:], start=True, stop=True)
-
         window_codes = patch_codes[:].bitcast(I32)
         window_scales = patch_scales[:].bitcast(I32)
         by_row = "p (r c) -> p r c"
@@ -234,51 +230,43 @@ def tile_conv2dkan_pa_s_kernel(
             )
         multiply(2 + 2 * PAIR, PAIR + 1)
         last_tap = TAPS - 2
-        halves = [slice(0, HALF_FILTERS), slice(HALF_FILTERS, FILTERS)]
         regroup(last_tap - 1)
-        for columns in halves:
-            regroup(last_tap, columns)
-        addend = keep.tile([ROWS, FILTERS], F32)
-        nc.scalar.copy(out=addend[:], in_=addend_ps[0:ROWS, :])
+        regroup(last_tap)
 
-        acc_0 = psum.tile([P, HALF_FILTERS], F32)
-        acc_1 = psum.tile([P, HALF_FILTERS], F32)
-        accs = [acc_0, acc_1]
-        def multiply_accumulate(tap, half):
+        acc = psum.tile([P, FILTERS], F32)
+
+        def multiply_accumulate(tap):
             nc.tensor.matmul_mx(
-                out=accs[half][:],
+                out=acc[:],
                 lhsT=patch_codes[:, tap, :].bitcast(FP8X4), lhsT_scale=patch_scales[:, tap, :],
-                rhs=weight_codes[:, tap, halves[half]].bitcast(FP8X4),
-                rhs_scale=weight_scales[:, tap, halves[half]],
+                rhs=weight_codes[:, tap, :].bitcast(FP8X4), rhs_scale=weight_scales[:, tap, :],
                 start=(tap == 0), stop=(tap == last_tap),
             )
 
-        for first, last in [(0, 2), (2, 4), (4, 6), (8, 9), (6, 7)]:
-            if first == 4:
-                regroup_on_vector(TAPS - 1)
-            if first > 0:
-                quantize(first, last, slice(0, FILTERS))
-            for tap in range(first, last):
-                for half in range(2):
-                    multiply_accumulate(tap, half)
-        for half in range(2):
-            quantize(last_tap, last_tap + 1, halves[half])
-            multiply_accumulate(last_tap, half)
+        multiply_accumulate(0)
+        multiply_accumulate(1)
+        quantize(2, 4)
+        multiply_accumulate(2)
+        multiply_accumulate(3)
+        regroup_on_vector(TAPS - 1)
+        quantize(4, 6)
+        multiply_accumulate(4)
+        multiply_accumulate(5)
+        addend_ps = psum.tile([P, FILTERS], F32)
+        nc.tensor.matmul(addend_ps[:], lhsT=pick[:], rhs=added[:], start=True, stop=True)
+        addend = keep.tile([ROWS, FILTERS], F32)
+        nc.scalar.copy(out=addend[:], in_=addend_ps[0:ROWS, :])
+        for tap in (8, 6, 7):
+            quantize(tap, tap + 1)
+            multiply_accumulate(tap)
 
         result = keep.tile([ROWS, FILTERS], F32)
+        nc.vector.tensor_tensor(out=result[:], in0=acc[0:ROWS, :], in1=addend[:], op=ALU.add)
         out_images = out.rearrange("b p q f -> b (p q) f")
         cut = STORE_SPLIT * IMAGES
         queues = [nc.sync, nc.scalar]
-        for half in range(2):
-            columns = halves[half]
-            nc.vector.tensor_tensor(
-                out=result[:, columns], in0=accs[half][0:ROWS, :], in1=addend[:, columns], op=ALU.add
+        for b in range(IMAGES):
+            queues[b].dma_start(out=out_images[b, 0:STORE_SPLIT, :], in_=result[b:cut:IMAGES, :])
+            queues[b].dma_start(
+                out=out_images[b, STORE_SPLIT:, :], in_=result[cut + b : ROWS : IMAGES, :]
             )
-            for b in range(IMAGES):
-                queues[b].dma_start(
-                    out=out_images[b, 0:STORE_SPLIT, columns], in_=result[b:cut:IMAGES, columns]
-                )
-                queues[b].dma_start(
-                    out=out_images[b, STORE_SPLIT:, columns],
-                    in_=result[cut + b : ROWS : IMAGES, columns],
-                )

@@ -19,6 +19,7 @@ KERNEL = 3
 TAPS = KERNEL * KERNEL
 OUT_SIDE = HEIGHT - KERNEL + 1
 FILTERS = 256
+HALF_FILTERS = FILTERS // 2
 POSITIONS = IMAGES * HEIGHT * WIDTH
 ROWS = IMAGES * OUT_SIDE * OUT_SIDE
 HALVES = 2
@@ -110,10 +111,10 @@ def tile_conv2dkan_pa_s_kernel(
                 op=ALU.mult,
             )
 
-        def regroup(tap):
+        def regroup(tap, columns=slice(0, FILTERS)):
             nc.scalar.copy(
-                out=grouped[:, tap].rearrange("p (c i) j -> p c j i", i=4),
-                in_=weight[:, tap].rearrange("p j (c i) -> p c j i", i=4),
+                out=grouped[:, tap, columns].rearrange("p (c i) j -> p c j i", i=4),
+                in_=weight[:, tap, :, columns].rearrange("p j (c i) -> p c j i", i=4),
             )
 
         def regroup_on_vector(tap):
@@ -128,11 +129,11 @@ def tile_conv2dkan_pa_s_kernel(
         weight_scales = keep.tile([P, TAPS, FILTERS], U8, align_bytes=64)
         join = "p t e -> p (t e)"
 
-        def quantize(first, last):
+        def quantize(first, last, columns=slice(0, FILTERS)):
             nc.vector.quantize_mx(
-                out=weight_codes[:, first:last, :].rearrange(join).bitcast(FP8X4),
-                scales=weight_scales[:, first:last, :].rearrange(join),
-                in_=grouped[:, first:last].rearrange("p t f j -> p (t f j)"),
+                out=weight_codes[:, first:last, columns].rearrange(join).bitcast(FP8X4),
+                scales=weight_scales[:, first:last, columns].rearrange(join),
+                in_=grouped[:, first:last, columns].rearrange("p t f j -> p (t f j)"),
             )
 
         centred = keep.tile([P, CHANNELS, HALVES], F32)
@@ -231,37 +232,51 @@ def tile_conv2dkan_pa_s_kernel(
         multiply(2 + 2 * PAIR, PAIR + 1)
         last_tap = TAPS - 2
         regroup(last_tap - 1)
-        regroup(last_tap)
+        halves = [slice(0, HALF_FILTERS), slice(HALF_FILTERS, FILTERS)]
+        for columns in halves:
+            regroup(last_tap, columns)
 
-        acc = psum.tile([P, FILTERS], F32)
+        acc_0 = psum.tile([P, HALF_FILTERS], F32)
+        acc_1 = psum.tile([P, HALF_FILTERS], F32)
+        accs = [acc_0, acc_1]
 
-        def multiply_accumulate(tap):
+        def multiply_accumulate(tap, half):
             nc.tensor.matmul_mx(
-                out=acc[:],
+                out=accs[half][:],
                 lhsT=patch_codes[:, tap, :].bitcast(FP8X4), lhsT_scale=patch_scales[:, tap, :],
-                rhs=weight_codes[:, tap, :].bitcast(FP8X4), rhs_scale=weight_scales[:, tap, :],
+                rhs=weight_codes[:, tap, halves[half]].bitcast(FP8X4),
+                rhs_scale=weight_scales[:, tap, halves[half]],
                 start=(tap == 0), stop=(tap == last_tap),
             )
 
-        multiply_accumulate(0)
-        multiply_accumulate(1)
-        quantize(2, 4)
-        multiply_accumulate(2)
-        multiply_accumulate(3)
-        regroup_on_vector(TAPS - 1)
-        quantize(4, 6)
-        multiply_accumulate(4)
-        multiply_accumulate(5)
+        def multiply_accumulate_taps(first, last):
+            for tap in range(first, last):
+                for half in range(2):
+                    multiply_accumulate(tap, half)
+
+        multiply_accumulate_taps(0, 2)
         addend_ps = psum.tile([P, FILTERS], F32)
         nc.tensor.matmul(addend_ps[:], lhsT=pick[:], rhs=added[:], start=True, stop=True)
         addend = keep.tile([ROWS, FILTERS], F32)
         nc.scalar.copy(out=addend[:], in_=addend_ps[0:ROWS, :])
-        for tap in (8, 6, 7):
+        quantize(2, 4)
+        multiply_accumulate_taps(2, 4)
+        regroup_on_vector(TAPS - 1)
+        quantize(4, 6)
+        multiply_accumulate_taps(4, 6)
+        for tap in (8, 6):
             quantize(tap, tap + 1)
-            multiply_accumulate(tap)
+            multiply_accumulate_taps(tap, tap + 1)
+        for half in range(2):
+            quantize(last_tap, last_tap + 1, halves[half])
+            multiply_accumulate(last_tap, half)
 
         result = keep.tile([ROWS, FILTERS], F32)
-        nc.vector.tensor_tensor(out=result[:], in0=acc[0:ROWS, :], in1=addend[:], op=ALU.add)
+        for half in range(2):
+            nc.vector.tensor_tensor(
+                out=result[:, halves[half]], in0=accs[half][0:ROWS, :], in1=addend[:, halves[half]],
+                op=ALU.add,
+            )
         out_images = out.rearrange("b p q f -> b (p q) f")
         cut = STORE_SPLIT * IMAGES
         queues = [nc.sync, nc.scalar]

@@ -26,6 +26,7 @@ HALVES = 2
 PAIR = 2
 IN_ROW = WIDTH * IMAGES
 OUT_ROW = OUT_SIDE * IMAGES
+WARM_TAPS, WARM_PASSES = 2, 2
 BYTES = 4
 BIAS_ROW = 96
 STORE_SPLIT = 32
@@ -259,6 +260,15 @@ def tile_conv2dkan_pa_s_kernel(
         nc.tensor.matmul(addend_ps[:], lhsT=pick[:], rhs=added[:], start=True, stop=True)
         addend = keep.tile([ROWS, FILTERS], F32)
         nc.scalar.copy(out=addend[:], in_=addend_ps[0:ROWS, :])
+        idle_ps = psum.tile([P, WARM_TAPS * FILTERS], F32)
+        for repeat in range(WARM_PASSES):
+            nc.tensor.matmul_mx(
+                out=idle_ps[:],
+                lhsT=patch_codes[:, 0, :].bitcast(FP8X4), lhsT_scale=patch_scales[:, 0, :],
+                rhs=weight_codes[:, 0:WARM_TAPS, :].rearrange(join).bitcast(FP8X4),
+                rhs_scale=weight_scales[:, 0:WARM_TAPS, :].rearrange(join),
+                start=True, stop=True,
+            )
         quantize(2, 4)
         multiply_accumulate_taps(2, 4)
         regroup_on_vector(TAPS - 1)

@@ -20,13 +20,15 @@ TAPS = KERNEL * KERNEL
 OUT_SIDE = HEIGHT - KERNEL + 1
 FILTERS = 256
 HALF_FILTERS = FILTERS // 2
-POSITIONS = IMAGES * HEIGHT * WIDTH
+PIXELS = HEIGHT * WIDTH
+POSITIONS = IMAGES * PIXELS
 ROWS = IMAGES * OUT_SIDE * OUT_SIDE
 HALVES = 2
+PLANE_HALVES = [slice(0, PACK // 2), slice(PACK // 2, PACK)]
 PAIR = 2
 IN_ROW = WIDTH * IMAGES
 OUT_ROW = OUT_SIDE * IMAGES
-WARM_TAPS, WARM_PASSES = 2, 2
+WARM_TAPS = 2
 BYTES = 4
 BIAS_ROW = 96
 STORE_SPLIT = 32
@@ -44,9 +46,7 @@ def tile_conv2dkan_pa_s_kernel(
         stack.enter_context(tc.manual_schedule())
 
         x_sb = keep.tile([P, CHANNELS], BF16)
-        x_images = x.rearrange("b h w c -> b (h w) c")
-        for b in range(IMAGES):
-            nc.scalar.dma_start(out=x_sb[b:P:IMAGES, :], in_=x_images[b])
+        nc.scalar.dma_start(out=x_sb[:], in_=x.rearrange("b h w c -> (b h w) c"))
         factor = keep.tile([P, TAPS, FILTERS], BF16)
         factor_rows = scale_factor.rearrange("(t c) f -> c t f", t=TAPS)
         raw = keep.tile([P, TAPS, PACK, FILTERS], BF16)
@@ -66,7 +66,10 @@ def tile_conv2dkan_pa_s_kernel(
                 in_=raw_rows[:, first:last, :],
             )
 
-        for first, last in [(0, 1), (1, 2), (2, 4), (4, 6), (6, TAPS)]:
+        load_factor(0, 2)
+        load_raw(0, 1)
+        load_raw(1, 2)
+        for first, last in [(2, 4), (4, 6), (6, TAPS)]:
             load_factor(first, last)
             load_raw(first, last)
 
@@ -75,6 +78,11 @@ def tile_conv2dkan_pa_s_kernel(
         nc.scalar.activation(out=warm[:], in_=warm[:], func=ACT.Abs)
         ident = keep.tile([P, P], F32)
         make_identity(nc, ident[:])
+        order = keep.tile([P, POSITIONS], F32)
+        for b in range(IMAGES):
+            nc.vector.tensor_copy(
+                out=order[:, b:POSITIONS:IMAGES], in_=ident[:, b * PIXELS : (b + 1) * PIXELS]
+            )
         pick = keep.tile([P, P], BF16)
         make_identity(nc, pick[:])
         nc.gpsimd.memset(pick[BIAS_ROW : BIAS_ROW + 2, :], 1.0)
@@ -118,8 +126,10 @@ def tile_conv2dkan_pa_s_kernel(
                 in_=weight[:, tap, :, columns].rearrange("p j (c i) -> p c j i", i=4),
             )
 
-        def regroup_on_vector(tap):
-            nc.vector.tensor_copy(out=grouped[:, tap], in_=weight[:, tap].rearrange("p j f -> p f j"))
+        def regroup_on_vector(tap, columns=slice(0, FILTERS)):
+            nc.vector.tensor_copy(
+                out=grouped[:, tap, columns], in_=weight[:, tap, :, columns].rearrange("p j f -> p f j")
+            )
 
         def multiply_and_regroup_pair(first):
             multiply(first, PAIR)
@@ -152,7 +162,11 @@ def tile_conv2dkan_pa_s_kernel(
                 bias=-float(j),
             )
         outer_sq = keep.tile(planes, F32)
-        nc.scalar.activation(out=outer_sq[:], in_=dist[:], func=ACT.Square, bias=2.0, scale=-1.0)
+        for planes_of_two in PLANE_HALVES:
+            nc.scalar.activation(
+                out=outer_sq[:, planes_of_two], in_=dist[:, planes_of_two], func=ACT.Square, bias=2.0,
+                scale=-1.0,
+            )
         inner_sq = keep.tile(planes, F32)
         nc.scalar.activation(out=inner_sq[:], in_=dist[:], func=ACT.Square, bias=1.0, scale=-1.0)
         multiply(0, 1)
@@ -179,20 +193,21 @@ def tile_conv2dkan_pa_s_kernel(
         for term in (outer_term, inner_term):
             for j in range(PACK):
                 nc.tensor.matmul(
-                    basis_ps[:, j, :], lhsT=term[:, j, :], rhs=ident[:], is_transpose=True,
+                    basis_ps[:, j, :], lhsT=term[:, j, :], rhs=order[:], is_transpose=True,
                     start=(term is outer_term and j == 0),
                     stop=(term is inner_term and j == PACK - 1),
                 )
-        multiply(2, PAIR)
+        multiply(2, 1)
+        multiply(3, 1)
         regroup(0)
         regroup(1)
         regroup(2)
-        regroup(3)
-        multiply_and_regroup_pair(2 + PAIR)
-        nc.vector.tensor_copy(
+        nc.scalar.copy(
             out=basis[:].rearrange("p (n j) -> p n j", j=PACK),
             in_=basis_ps[:].rearrange("p j n -> p n j"),
         )
+        regroup(3)
+        multiply_and_regroup_pair(2 + PAIR)
         quantize(0, 2)
         nc.vector.quantize_mx(
             out=basis_codes[:].bitcast(FP8X4), scales=basis_scales[:], in_=basis[:]
@@ -234,8 +249,7 @@ def tile_conv2dkan_pa_s_kernel(
         last_tap = TAPS - 2
         regroup(last_tap - 1)
         halves = [slice(0, HALF_FILTERS), slice(HALF_FILTERS, FILTERS)]
-        for columns in halves:
-            regroup(last_tap, columns)
+        regroup(last_tap, halves[0])
 
         acc_0 = psum.tile([P, HALF_FILTERS], F32)
         acc_1 = psum.tile([P, HALF_FILTERS], F32)
@@ -255,34 +269,41 @@ def tile_conv2dkan_pa_s_kernel(
                 for half in range(2):
                     multiply_accumulate(tap, half)
 
+        idle_ps = psum.tile([P, WARM_TAPS * FILTERS], F32)
+
+        def keep_busy(passes):
+            for repeat in range(passes):
+                nc.tensor.matmul_mx(
+                    out=idle_ps[:],
+                    lhsT=weight_codes[:, 0, 0:P].bitcast(FP8X4), lhsT_scale=weight_scales[:, 0, 0:P],
+                    rhs=weight_codes[:, 0:WARM_TAPS, :].rearrange(join).bitcast(FP8X4),
+                    rhs_scale=weight_scales[:, 0:WARM_TAPS, :].rearrange(join),
+                    start=True, stop=True,
+                )
+
+        keep_busy(2)
         multiply_accumulate_taps(0, 2)
         addend_ps = psum.tile([P, FILTERS], F32)
         nc.tensor.matmul(addend_ps[:], lhsT=pick[:], rhs=added[:], start=True, stop=True)
         addend = keep.tile([ROWS, FILTERS], F32)
         nc.scalar.copy(out=addend[:], in_=addend_ps[0:ROWS, :])
-        idle_ps = psum.tile([P, WARM_TAPS * FILTERS], F32)
-        for repeat in range(WARM_PASSES):
-            nc.tensor.matmul_mx(
-                out=idle_ps[:],
-                lhsT=patch_codes[:, 0, :].bitcast(FP8X4), lhsT_scale=patch_scales[:, 0, :],
-                rhs=weight_codes[:, 0:WARM_TAPS, :].rearrange(join).bitcast(FP8X4),
-                rhs_scale=weight_scales[:, 0:WARM_TAPS, :].rearrange(join),
-                start=True, stop=True,
-            )
+        keep_busy(2)
         quantize(2, 4)
         multiply_accumulate_taps(2, 4)
+        keep_busy(1)
         regroup_on_vector(TAPS - 1)
         quantize(4, 6)
         multiply_accumulate_taps(4, 6)
+        regroup_on_vector(last_tap, halves[1])
         for tap in (8, 6):
             quantize(tap, tap + 1)
             multiply_accumulate_taps(tap, tap + 1)
-        for half in range(2):
+        for half in (1, 0):
             quantize(last_tap, last_tap + 1, halves[half])
             multiply_accumulate(last_tap, half)
 
         result = keep.tile([ROWS, FILTERS], F32)
-        for half in range(2):
+        for half in (1, 0):
             nc.vector.tensor_tensor(
                 out=result[:, halves[half]], in0=accs[half][0:ROWS, :], in1=addend[:, halves[half]],
                 op=ALU.add,

@@ -281,7 +281,6 @@ def tile_conv2dkan_pa_s_kernel(
                     start=True, stop=True,
                 )
 
-        keep_busy(2)
         multiply_accumulate_taps(0, 2)
         addend_ps = psum.tile([P, FILTERS], F32)
         nc.tensor.matmul(addend_ps[:], lhsT=pick[:], rhs=added[:], start=True, stop=True)
@@ -290,7 +289,6 @@ def tile_conv2dkan_pa_s_kernel(
         keep_busy(2)
         quantize(2, 4)
         multiply_accumulate_taps(2, 4)
-        keep_busy(1)
         regroup_on_vector(TAPS - 1)
         quantize(4, 6)
         multiply_accumulate_taps(4, 6)

@@ -69,9 +69,12 @@ def tile_conv2dkan_pa_s_kernel(
         load_factor(0, 2)
         load_raw(0, 1)
         load_raw(1, 2)
-        for first, last in [(2, 4), (4, 6), (6, TAPS)]:
+        for first, last in [(2, 4), (4, 6)]:
             load_factor(first, last)
             load_raw(first, last)
+        load_factor(6, TAPS)
+        for tap in range(6, TAPS):
+            load_raw(tap, tap + 1)
 
         warm = keep.tile([P, 1], F32)
         nc.vector.memset(warm[:], 0.0)
@@ -245,7 +248,10 @@ def tile_conv2dkan_pa_s_kernel(
                 out=window_scales[:, taps, 0 : ROWS // BYTES],
                 in_=window_scales[:, 0:KERNEL, start // BYTES : (start + ROWS) // BYTES],
             )
-        multiply(2 + 2 * PAIR, PAIR + 1)
+        multiply(6, 1)
+        quantize(2, 4)
+        multiply(7, 1)
+        multiply(8, 1)
         last_tap = TAPS - 2
         regroup(last_tap - 1)
         halves = [slice(0, HALF_FILTERS), slice(HALF_FILTERS, FILTERS)]
@@ -286,9 +292,9 @@ def tile_conv2dkan_pa_s_kernel(
         nc.tensor.matmul(addend_ps[:], lhsT=pick[:], rhs=added[:], start=True, stop=True)
         addend = keep.tile([ROWS, FILTERS], F32)
         nc.scalar.copy(out=addend[:], in_=addend_ps[0:ROWS, :])
+        multiply_accumulate_taps(2, 3)
         keep_busy(2)
-        quantize(2, 4)
-        multiply_accumulate_taps(2, 4)
+        multiply_accumulate_taps(3, 4)
         regroup_on_vector(TAPS - 1)
         quantize(4, 6)
         multiply_accumulate_taps(4, 6)

@@ -20,8 +20,7 @@ TAPS = KERNEL * KERNEL
 OUT_SIDE = HEIGHT - KERNEL + 1
 FILTERS = 256
 HALF_FILTERS = FILTERS // 2
-PIXELS = HEIGHT * WIDTH
-POSITIONS = IMAGES * PIXELS
+POSITIONS = IMAGES * HEIGHT * WIDTH
 ROWS = IMAGES * OUT_SIDE * OUT_SIDE
 HALVES = 2
 PLANE_HALVES = [slice(0, PACK // 2), slice(PACK // 2, PACK)]
@@ -46,7 +45,9 @@ def tile_conv2dkan_pa_s_kernel(
         stack.enter_context(tc.manual_schedule())
 
         x_sb = keep.tile([P, CHANNELS], BF16)
-        nc.scalar.dma_start(out=x_sb[:], in_=x.rearrange("b h w c -> (b h w) c"))
+        x_images = x.rearrange("b h w c -> b (h w) c")
+        for b in range(IMAGES):
+            nc.scalar.dma_start(out=x_sb[b:P:IMAGES, :], in_=x_images[b])
         factor = keep.tile([P, TAPS, FILTERS], BF16)
         factor_rows = scale_factor.rearrange("(t c) f -> c t f", t=TAPS)
         raw = keep.tile([P, TAPS, PACK, FILTERS], BF16)
@@ -81,14 +82,8 @@ def tile_conv2dkan_pa_s_kernel(
         nc.scalar.activation(out=warm[:], in_=warm[:], func=ACT.Abs)
         ident = keep.tile([P, P], F32)
         make_identity(nc, ident[:])
-        order = keep.tile([P, POSITIONS], F32)
-        for b in range(IMAGES):
-            nc.vector.tensor_copy(
-                out=order[:, b:POSITIONS:IMAGES], in_=ident[:, b * PIXELS : (b + 1) * PIXELS]
-            )
         pick = keep.tile([P, P], BF16)
-        make_identity(nc, pick[:])
-        nc.gpsimd.memset(pick[BIAS_ROW : BIAS_ROW + 2, :], 1.0)
+        nc.scalar.copy(out=pick[:], in_=ident[:])
         half_shift = keep.tile([P, HALVES], F32)
         for h in range(HALVES):
             nc.vector.memset(half_shift[:, h : h + 1], 3.5 - PACK * h)
@@ -103,6 +98,7 @@ def tile_conv2dkan_pa_s_kernel(
         nc.gpsimd.dma_start(
             out=added[BIAS_ROW + 1 : BIAS_ROW + 2, :], in_=conv_bias.rearrange("(o f) -> o f", o=1)
         )
+        nc.gpsimd.memset(pick[BIAS_ROW : BIAS_ROW + 2, :], 1.0)
         basis = keep.tile([P, POSITIONS * PACK], BF16, align_bytes=64)
         basis_codes = keep.tile([P, POSITIONS], U32, align_bytes=64)
         basis_scales = keep.tile([P, POSITIONS], U8, align_bytes=64)
@@ -129,10 +125,8 @@ def tile_conv2dkan_pa_s_kernel(
                 in_=weight[:, tap, :, columns].rearrange("p j (c i) -> p c j i", i=4),
             )
 
-        def regroup_on_vector(tap, columns=slice(0, FILTERS)):
-            nc.vector.tensor_copy(
-                out=grouped[:, tap, columns], in_=weight[:, tap, :, columns].rearrange("p j f -> p f j")
-            )
+        def regroup_on_vector(tap):
+            nc.vector.tensor_copy(out=grouped[:, tap], in_=weight[:, tap].rearrange("p j f -> p f j"))
 
         def multiply_and_regroup_pair(first):
             multiply(first, PAIR)
@@ -196,7 +190,7 @@ def tile_conv2dkan_pa_s_kernel(
         for term in (outer_term, inner_term):
             for j in range(PACK):
                 nc.tensor.matmul(
-                    basis_ps[:, j, :], lhsT=term[:, j, :], rhs=order[:], is_transpose=True,
+                    basis_ps[:, j, :], lhsT=term[:, j, :], rhs=ident[:], is_transpose=True,
                     start=(term is outer_term and j == 0),
                     stop=(term is inner_term and j == PACK - 1),
                 )
@@ -255,7 +249,8 @@ def tile_conv2dkan_pa_s_kernel(
         last_tap = TAPS - 2
         regroup(last_tap - 1)
         halves = [slice(0, HALF_FILTERS), slice(HALF_FILTERS, FILTERS)]
-        regroup(last_tap, halves[0])
+        for columns in halves:
+            regroup(last_tap, columns)
 
         acc_0 = psum.tile([P, HALF_FILTERS], F32)
         acc_1 = psum.tile([P, HALF_FILTERS], F32)
@@ -298,16 +293,15 @@ def tile_conv2dkan_pa_s_kernel(
         regroup_on_vector(TAPS - 1)
         quantize(4, 6)
         multiply_accumulate_taps(4, 6)
-        regroup_on_vector(last_tap, halves[1])
         for tap in (8, 6):
             quantize(tap, tap + 1)
             multiply_accumulate_taps(tap, tap + 1)
-        for half in (1, 0):
+        for half in range(2):
             quantize(last_tap, last_tap + 1, halves[half])
             multiply_accumulate(last_tap, half)
 
         result = keep.tile([ROWS, FILTERS], F32)
-        for half in (1, 0):
+        for half in range(2):
             nc.vector.tensor_tensor(
                 out=result[:, halves[half]], in0=accs[half][0:ROWS, :], in1=addend[:, halves[half]],
                 op=ALU.add,

from contextlib import ExitStack

import concourse.mybir as mybir
from concourse.masks import make_identity

F32 = mybir.dt.float32
BF16 = mybir.dt.bfloat16
I32 = mybir.dt.int32
U32 = mybir.dt.uint32
U8 = mybir.dt.uint8
FP8X4 = mybir.dt.float8_e4m3fn_x4
ALU = mybir.AluOpType
ACT = mybir.ActivationFunctionType

P = 128
PACK = 4
IMAGES, HEIGHT, WIDTH, CHANNELS = 2, 8, 8, 64
KERNEL = 3
TAPS = KERNEL * KERNEL
OUT_SIDE = HEIGHT - KERNEL + 1
FILTERS = 256
HALF_FILTERS = FILTERS // 2
POSITIONS = IMAGES * HEIGHT * WIDTH
ROWS = IMAGES * OUT_SIDE * OUT_SIDE
HALVES = 2
PLANE_HALVES = [slice(0, PACK // 2), slice(PACK // 2, PACK)]
PAIR = 2
IN_ROW = WIDTH * IMAGES
OUT_ROW = OUT_SIDE * IMAGES
WARM_TAPS = 2
BYTES = 4
BIAS_ROW = 96
STORE_SPLIT = 32

FLOPS = 2 * ROWS * TAPS * CHANNELS * 8 * FILTERS


def tile_conv2dkan_pa_s_kernel(
    tc, x, spline_kernel, scale_factor, base, kan_bias, conv_bias, out
):
    nc = tc.nc
    with ExitStack() as stack:
        keep = stack.enter_context(tc.tile_pool(name="keep", bufs=1))
        psum = stack.enter_context(tc.psum_pool(name="psum", bufs=1))
        stack.enter_context(tc.manual_schedule())

        x_sb = keep.tile([P, CHANNELS], BF16)
        x_images = x.rearrange("b h w c -> b (h w) c")
        for b in range(IMAGES):
            nc.scalar.dma_start(out=x_sb[b:P:IMAGES, :], in_=x_images[b])
        factor = keep.tile([P, TAPS, FILTERS], BF16)
        factor_rows = scale_factor.rearrange("(t c) f -> c t f", t=TAPS)
        raw = keep.tile([P, TAPS, PACK, FILTERS], BF16)
        raw_rows = spline_kernel.rearrange("(t c) k f -> t (c k) f", t=TAPS).rearrange(
            "t (p j) f -> p t (j f)", j=PACK
        )

        def load_factor(first, last):
            for h in range(HALVES):
                nc.sync.dma_start(
                    out=factor[h:P:HALVES, first:last, :], in_=factor_rows[:, first:last, :]
                )

        def load_raw(first, last):
            nc.sync.dma_start(
                out=raw[:, first:last].rearrange("p t j f -> p t (j f)"),
                in_=raw_rows[:, first:last, :],
            )

        load_factor(0, 2)
        load_raw(0, 1)
        load_raw(1, 2)
        for first, last in [(2, 4), (4, 6)]:
            load_factor(first, last)
            load_raw(first, last)
        load_factor(6, TAPS)
        for tap in range(6, TAPS):
            load_raw(tap, tap + 1)

        warm = keep.tile([P, 1], F32)
        nc.vector.memset(warm[:], 0.0)
        nc.scalar.activation(out=warm[:], in_=warm[:], func=ACT.Abs)
        ident = keep.tile([P, P], F32)
        make_identity(nc, ident[:])
        pick = keep.tile([P, P], BF16)
        nc.scalar.copy(out=pick[:], in_=ident[:])
        half_shift = keep.tile([P, HALVES], F32)
        for h in range(HALVES):
            nc.vector.memset(half_shift[:, h : h + 1], 3.5 - PACK * h)
        added = keep.tile([P, FILTERS], BF16)
        nc.vector.memset(added[:].bitcast(I32), 0)
        base_images = base.rearrange("b p q f -> b (p q) f")
        for b in range(IMAGES):
            nc.gpsimd.dma_start(out=added[b:ROWS:IMAGES, :], in_=base_images[b])
        nc.gpsimd.dma_start(
            out=added[BIAS_ROW : BIAS_ROW + 1, :], in_=kan_bias.rearrange("(o f) -> o f", o=1)
        )
        nc.gpsimd.dma_start(
            out=added[BIAS_ROW + 1 : BIAS_ROW + 2, :], in_=conv_bias.rearrange("(o f) -> o f", o=1)
        )
        nc.gpsimd.memset(pick[BIAS_ROW : BIAS_ROW + 2, :], 1.0)
        basis = keep.tile([P, POSITIONS * PACK], BF16, align_bytes=64)
        basis_codes = keep.tile([P, POSITIONS], U32, align_bytes=64)
        basis_scales = keep.tile([P, POSITIONS], U8, align_bytes=64)
        nc.vector.memset(basis_scales[:].bitcast(I32), 0)
        patch_codes = keep.tile([P, TAPS, P], U32, align_bytes=64)
        patch_scales = keep.tile([P, TAPS, P], U8, align_bytes=64)
        nc.vector.memset(patch_codes[:].bitcast(I32)[:, :, ROWS:], 0)
        nc.vector.memset(patch_scales[:].bitcast(I32), 0)

        weight = keep.tile([P, TAPS, PACK, FILTERS], BF16)
        grouped = keep.tile([P, TAPS, FILTERS, PACK], BF16, align_bytes=64)

        def multiply(first, count):
            taps = slice(first, first + count)
            nc.vector.tensor_tensor(
                out=weight[:, taps], in0=raw[:, taps],
                in1=factor[:, taps, :].unsqueeze(2).to_broadcast([P, count, PACK, FILTERS]),
                op=ALU.mult,
            )

        def regroup(tap, columns=slice(0, FILTERS)):
            nc.scalar.copy(
                out=grouped[:, tap, columns].rearrange("p (c i) j -> p c j i", i=4),
                in_=weight[:, tap, :, columns].rearrange("p j (c i) -> p c j i", i=4),
            )

        def regroup_on_vector(tap):
            nc.vector.tensor_copy(out=grouped[:, tap], in_=weight[:, tap].rearrange("p j f -> p f j"))

        def multiply_and_regroup_pair(first):
            multiply(first, PAIR)
            for tap in range(first, first + PAIR):
                regroup(tap)

        weight_codes = keep.tile([P, TAPS, FILTERS], U32, align_bytes=64)
        weight_scales = keep.tile([P, TAPS, FILTERS], U8, align_bytes=64)
        join = "p t e -> p (t e)"

        def quantize(first, last, columns=slice(0, FILTERS)):
            nc.vector.quantize_mx(
                out=weight_codes[:, first:last, columns].rearrange(join).bitcast(FP8X4),
                scales=weight_scales[:, first:last, columns].rearrange(join),
                in_=grouped[:, first:last, columns].rearrange("p t f j -> p (t f j)"),
            )

        centred = keep.tile([P, CHANNELS, HALVES], F32)
        nc.vector.scalar_tensor_tensor(
            out=centred[:], in0=x_sb[:].unsqueeze(2).to_broadcast([P, CHANNELS, HALVES]), scalar=2.5,
            in1=half_shift[:].unsqueeze(1).to_broadcast([P, CHANNELS, HALVES]),
            op0=ALU.mult, op1=ALU.add,
        )
        planes = [P, PACK, P]
        flat = "p j m -> p (j m)"
        dist = keep.tile(planes, F32)
        for j in range(PACK):
            nc.scalar.activation(
                out=dist[:, j, :], in_=centred[:].rearrange("p c h -> p (c h)"), func=ACT.Abs,
                bias=-float(j),
            )
        outer_sq = keep.tile(planes, F32)
        for planes_of_two in PLANE_HALVES:
            nc.scalar.activation(
                out=outer_sq[:, planes_of_two], in_=dist[:, planes_of_two], func=ACT.Square, bias=2.0,
                scale=-1.0,
            )
        inner_sq = keep.tile(planes, F32)
        nc.scalar.activation(out=inner_sq[:], in_=dist[:], func=ACT.Square, bias=1.0, scale=-1.0)
        multiply(0, 1)
        outer_neg = keep.tile(planes, F32)
        nc.vector.tensor_scalar(
            out=outer_neg[:], in0=dist[:], scalar1=2.0, scalar2=-2.0, op0=ALU.min, op1=ALU.add
        )
        inner_neg = keep.tile(planes, F32)
        nc.vector.tensor_scalar(
            out=inner_neg[:], in0=dist[:], scalar1=1.0, scalar2=-1.0, op0=ALU.min, op1=ALU.add
        )
        multiply(1, 1)
        outer_term = keep.tile(planes, F32)
        nc.vector.scalar_tensor_tensor(
            out=outer_term[:].rearrange(flat), in0=outer_sq[:].rearrange(flat), scalar=-1.0 / 6.0,
            in1=outer_neg[:].rearrange(flat), op0=ALU.mult, op1=ALU.mult,
        )
        inner_term = keep.tile(planes, F32)
        nc.vector.scalar_tensor_tensor(
            out=inner_term[:].rearrange(flat), in0=inner_sq[:].rearrange(flat), scalar=2.0 / 3.0,
            in1=inner_neg[:].rearrange(flat), op0=ALU.mult, op1=ALU.mult,
        )
        basis_ps = psum.tile([P, PACK, POSITIONS], F32)
        for term in (outer_term, inner_term):
            for j in range(PACK):
                nc.tensor.matmul(
                    basis_ps[:, j, :], lhsT=term[:, j, :], rhs=ident[:], is_transpose=True,
                    start=(term is outer_term and j == 0),
                    stop=(term is inner_term and j == PACK - 1),
                )
        multiply(2, 1)
        multiply(3, 1)
        regroup(0)
        regroup(1)
        regroup(2)
        nc.scalar.copy(
            out=basis[:].rearrange("p (n j) -> p n j", j=PACK),
            in_=basis_ps[:].rearrange("p j n -> p n j"),
        )
        regroup(3)
        multiply_and_regroup_pair(2 + PAIR)
        quantize(0, 2)
        nc.vector.quantize_mx(
            out=basis_codes[:].bitcast(FP8X4), scales=basis_scales[:], in_=basis[:]
        )
        window_codes = patch_codes[:].bitcast(I32)
        window_scales = patch_scales[:].bitcast(I32)
        by_row = "p (r c) -> p r c"
        code_rows = basis_codes[:].bitcast(I32).rearrange(by_row, r=HEIGHT)
        scale_rows = basis_scales[:].rearrange(by_row, r=HEIGHT)
        scale_word_rows = basis_scales[:].bitcast(I32).rearrange(by_row, r=HEIGHT)
        narrow = HEIGHT * OUT_ROW
        for dj in range(KERNEL):
            shift = dj * IMAGES
            nc.vector.tensor_copy(
                out=window_codes[:, dj, 0:narrow].rearrange(by_row, r=HEIGHT),
                in_=code_rows[:, :, shift : shift + OUT_ROW],
            )
            if shift % BYTES == 0:
                nc.vector.tensor_copy(
                    out=window_scales[:, dj, 0 : narrow // BYTES].rearrange(by_row, r=HEIGHT),
                    in_=scale_word_rows[:, :, shift // BYTES : (shift + OUT_ROW) // BYTES],
                )
            else:
                nc.vector.tensor_copy(
                    out=patch_scales[:, dj, 0:narrow].rearrange(by_row, r=HEIGHT),
                    in_=scale_rows[:, :, shift : shift + OUT_ROW],
                )
        for di in range(1, KERNEL):
            taps = slice(di * KERNEL, (di + 1) * KERNEL)
            start = di * OUT_ROW
            nc.sync.dma_start(
                out=window_codes[:, taps, 0:ROWS], in_=window_codes[:, 0:KERNEL, start : start + ROWS]
            )
            nc.sync.dma_start(
                out=window_scales[:, taps, 0 : ROWS // BYTES],
                in_=window_scales[:, 0:KERNEL, start // BYTES : (start + ROWS) // BYTES],
            )
        multiply(6, 1)
        quantize(2, 4)
        multiply(7, 1)
        multiply(8, 1)
        last_tap = TAPS - 2
        regroup(last_tap - 1)
        halves = [slice(0, HALF_FILTERS), slice(HALF_FILTERS, FILTERS)]
        for columns in halves:
            regroup(last_tap, columns)

        acc_0 = psum.tile([P, HALF_FILTERS], F32)
        acc_1 = psum.tile([P, HALF_FILTERS], F32)
        accs = [acc_0, acc_1]

        def multiply_accumulate(tap, half):
            nc.tensor.matmul_mx(
                out=accs[half][:],
                lhsT=patch_codes[:, tap, :].bitcast(FP8X4), lhsT_scale=patch_scales[:, tap, :],
                rhs=weight_codes[:, tap, halves[half]].bitcast(FP8X4),
                rhs_scale=weight_scales[:, tap, halves[half]],
                start=(tap == 0), stop=(tap == last_tap),
            )

        def multiply_accumulate_taps(first, last):
            for tap in range(first, last):
                for half in range(2):
                    multiply_accumulate(tap, half)

        idle_ps = psum.tile([P, WARM_TAPS * FILTERS], F32)

        def keep_busy(passes):
            for repeat in range(passes):
                nc.tensor.matmul_mx(
                    out=idle_ps[:],
                    lhsT=weight_codes[:, 0, 0:P].bitcast(FP8X4), lhsT_scale=weight_scales[:, 0, 0:P],
                    rhs=weight_codes[:, 0:WARM_TAPS, :].rearrange(join).bitcast(FP8X4),
                    rhs_scale=weight_scales[:, 0:WARM_TAPS, :].rearrange(join),
                    start=True, stop=True,
                )

        multiply_accumulate_taps(0, 2)
        addend_ps = psum.tile([P, FILTERS], F32)
        nc.tensor.matmul(addend_ps[:], lhsT=pick[:], rhs=added[:], start=True, stop=True)
        addend = keep.tile([ROWS, FILTERS], F32)
        nc.scalar.copy(out=addend[:], in_=addend_ps[0:ROWS, :])
        multiply_accumulate_taps(2, 3)
        keep_busy(2)
        multiply_accumulate_taps(3, 4)
        regroup_on_vector(TAPS - 1)
        quantize(4, 6)
        multiply_accumulate_taps(4, 6)
        for tap in (8, 6):
            quantize(tap, tap + 1)
            multiply_accumulate_taps(tap, tap + 1)
        for half in range(2):
            quantize(last_tap, last_tap + 1, halves[half])
            multiply_accumulate(last_tap, half)

        result = keep.tile([ROWS, FILTERS], F32)
        for half in range(2):
            nc.vector.tensor_tensor(
                out=result[:, halves[half]], in0=accs[half][0:ROWS, :], in1=addend[:, halves[half]],
                op=ALU.add,
            )
        out_images = out.rearrange("b p q f -> b (p q) f")
        cut = STORE_SPLIT * IMAGES
        queues = [nc.sync, nc.scalar]
        for b in range(IMAGES):
            queues[b].dma_start(out=out_images[b, 0:STORE_SPLIT, :], in_=result[b:cut:IMAGES, :])
            queues[b].dma_start(
                out=out_images[b, STORE_SPLIT:, :], in_=result[cut + b : ROWS : IMAGES, :]
            )
